import numpy as np
import ml_dtypes


def mxq(x, axis, fmt="e4m3"):
    dtype, down = {"e4m3": (ml_dtypes.float8_e4m3fn, 7), "e5m2": (ml_dtypes.float8_e5m2, 14)}[fmt]
    v = np.moveaxis(np.asarray(x, np.float32).astype(ml_dtypes.bfloat16).astype(np.float64), axis, -1)
    blocks = v.reshape(v.shape[:-1] + (-1, 32))
    amax = np.abs(blocks).max(-1, keepdims=True)
    byte = np.maximum(np.where(amax > 0, np.frexp(amax)[1] - 1 + 127, 0) - down, 1)
    scale = np.exp2(byte - 127.0)
    codes = (blocks / scale).astype(np.float32).astype(dtype).astype(np.float64)
    return np.moveaxis((codes * scale).reshape(v.shape), -1, axis)


WIDE = False


def mx_kscale(k):
    if not WIDE:
        return np.ones(k)
    levels = np.array([10, -10, 5, -5, 0])
    a = np.random.permutation(np.resize(levels, k // 512 * 4)).reshape(k // 512, 4)
    idx = np.arange(k)
    return np.exp2(a[idx // 512, idx % 128 // 32])


BF16 = ml_dtypes.bfloat16


def bf(x):
    return np.asarray(x, np.float32).astype(BF16)


def f64(x):
    return np.asarray(x).astype(np.float64)


E2M1 = np.array([0.0, 0.5, 1.0, 1.5, 2.0, 3.0, 4.0, 6.0, -0.0, -0.5, -1.0, -1.5, -2.0, -3.0, -4.0, -6.0])


def pack_weight(w, fmt):
    k, n = w.shape
    w = f64(bf(w)).reshape(k // 32, 32, n)
    amax = np.abs(w).max(1)
    if fmt == "e4m3":
        byte = np.frexp(amax)[1] - 1 + 127 - 7
    else:
        mant, ex = np.frexp(amax / 6.0)
        byte = np.where(mant > 0.5, ex, ex - 1) + 127
    byte = np.clip(np.where(amax > 0, byte, 1), 1, 254)
    scaled = (w * np.exp2(127.0 - byte)[:, None, :]).reshape(k, n).astype(np.float32)
    by_word = np.ascontiguousarray(scaled.reshape(k // 512, 128, 4, n).transpose(0, 1, 3, 2))
    if fmt == "e4m3":
        words = by_word.astype(ml_dtypes.float8_e4m3fn).view(np.uint8)
    else:
        c = by_word.astype(ml_dtypes.float4_e2m1fn).view(np.uint8) & 0xF
        words = c[..., 0::2] | (c[..., 1::2] << 4)
    return np.ascontiguousarray(words), np.ascontiguousarray(byte.astype(np.uint8).reshape(k // 512, 16, n))


def unpack_weight(words, scales, fmt):
    g, p, n, _ = words.shape
    if fmt == "e4m3":
        vals = np.ascontiguousarray(words).view(ml_dtypes.float8_e4m3fn).astype(np.float64)
    else:
        nib = np.empty((g, p, n, 4), np.uint8)
        nib[..., 0::2] = words & 0xF
        nib[..., 1::2] = words >> 4
        vals = E2M1[nib]
    vals = vals * np.repeat(np.exp2(scales.astype(np.float64) - 127.0), 8, axis=1)[..., None]
    return vals.transpose(0, 1, 3, 2).reshape(g * 512, n)

def pack4(w):
    words, scales = pack_weight(w, "e2m1")
    return words.reshape(words.shape[0], 128, -1), scales


def unpack4(words, scales):
    return unpack_weight(words.reshape(words.shape[0], 128, -1, 2), scales, "e2m1")


B, D, S, N = 4096, 1024, 2, 128
DS = D // S


def sigmoid(v):
    return 1.0 / (1.0 + np.exp(-v))


def setup_inputs():
    s = mx_kscale(D)
    t = np.maximum(1.0 + 2.0 * np.random.standard_normal((B, N, S)), 0.0) + np.maximum(1.0 + 2.0 * np.random.standard_normal((B, N, S)), 0.0)
    a = bf(t * t / (t * t).sum(axis=1, keepdims=True))
    vr = bf(np.random.standard_normal((N, S, DS)) * 0.5 * np.sqrt(N) * s.reshape(S, DS))
    h = bf(np.random.standard_normal((B, D)) * s)
    x2g = bf(np.random.standard_normal((B, D)))
    w_g = np.random.standard_normal((D, D)) / np.sqrt(D) / s
    w_g_words, w_g_scales = pack4(np.ascontiguousarray(w_g.T))
    b_g = bf(np.random.standard_normal(D) * 0.3)
    bg = bf(1.0 + 0.1 * np.random.standard_normal(1))
    return {"a": a,
            "vr": vr,
            "h": h,
            "x2g": x2g,
            "w_g_words": w_g_words,
            "w_g_scales": w_g_scales,
            "b_g": b_g,
            "bg": bg}


def reference(a, vr, h, x2g, w_g_words, w_g_scales, b_g, bg):
    hf = f64(h)
    hh = (f64(a).transpose(2, 0, 1) @ f64(vr).transpose(1, 0, 2)).transpose(1, 0, 2).reshape(B, D)
    h2g = (mxq(hf, 1, "e4m3") @ unpack4(w_g_words, w_g_scales)) + f64(b_g)
    g = sigmoid(f64(x2g) + h2g + f64(bg))
    return g * hh + (1.0 - g) * hf

@@ -1,0 +1,146 @@
+from contextlib import ExitStack
+
+import concourse.mybir as mybir
+from concourse.masks import make_identity
+
+F32 = mybir.dt.float32
+BF16 = mybir.dt.bfloat16
+I32 = mybir.dt.int32
+U32 = mybir.dt.uint32
+U8 = mybir.dt.uint8
+FP8X4 = mybir.dt.float8_e4m3fn_x4
+FP4X4 = mybir.dt.float4_e2m1fn_x4
+ALU = mybir.AluOpType
+ACT = mybir.ActivationFunctionType
+
+B, D, S, N = 4096, 1024, 2, 128
+DS = D // S
+P = 128
+G = D // 512
+J = 4
+CHUNKS = B // (P * J)
+ROW_TILES = CHUNKS * J
+AHEAD = 2
+
+FLOPS = 2 * B * D * D + 2 * B * N * D
+
+
+def tile_tpru_pb_t_kernel(tc, a, vr, h, x2g, w_g_words, w_g_scales, b_g, bg, out):
+    nc = tc.nc
+    h_chunks = h.rearrange("(c p j) k -> c p j k", p=P, j=J)
+    x_chunks = x2g.rearrange("(c p j) k -> c p j k", p=P, j=J)
+    a_chunks = a.rearrange("(c p j) n s -> c p j (n s)", p=P, j=J)
+    out_chunks = out.rearrange("(c p j) k -> c p j k", p=P, j=J)
+
+    with ExitStack() as ctx:
+        const = ctx.enter_context(tc.tile_pool(name="const", bufs=1))
+        loads = ctx.enter_context(tc.tile_pool(name="loads", bufs=3))
+        quant = ctx.enter_context(tc.tile_pool(name="quant", bufs=AHEAD + 2))
+        work = ctx.enter_context(tc.tile_pool(name="work", bufs=3))
+        psum_t = ctx.enter_context(tc.psum_pool(name="psum_t", bufs=2))
+        psum_z = ctx.enter_context(tc.psum_pool(name="psum_z", bufs=3))
+        psum_h = ctx.enter_context(tc.psum_pool(name="psum_h", bufs=3))
+
+        h_tiles, x_tiles, a_tiles, aT_tiles = {}, {}, {}, {}
+        code_tiles, scale_tiles = {}, {}
+
+        def load_chunk(c):
+            h_sb = loads.tile([P, J, D], BF16, name="h_sb")
+            nc.sync.dma_start(out=h_sb[:], in_=h_chunks[c])
+            a_sb = loads.tile([P, J, N * S], BF16, name="a_sb")
+            nc.sync.dma_start(out=a_sb[:], in_=a_chunks[c])
+            x_sb = loads.tile([P, J, D], BF16, name="x_sb")
+            nc.sync.dma_start(out=x_sb[:], in_=x_chunks[c])
+            h_tiles[c], a_tiles[c], x_tiles[c] = h_sb, a_sb, x_sb
+
+        load_chunk(0)
+
+        ident = const.tile([P, P], F32)
+        make_identity(nc, ident[:])
+
+        w_words = const.tile([P, G, 2 * D], U8, align_bytes=64)
+        nc.sync.dma_start(
+            out=w_words[:].bitcast(I32), in_=w_g_words.rearrange("g p c -> p g c").bitcast(I32)
+        )
+        w_planes = const.tile([P, G, D], U8, align_bytes=64)
+        nc.vector.memset(w_planes[:].bitcast(I32), 0)
+        for quad in range(4):
+            nc.sync.dma_start(
+                out=w_planes[32 * quad : 32 * quad + 4].bitcast(I32),
+                in_=w_g_scales[:, 4 * quad : 4 * quad + 4, :].rearrange("g r n -> r g n").bitcast(I32),
+            )
+        vr_sb = const.tile([P, S, DS], BF16)
+        nc.sync.dma_start(out=vr_sb[:], in_=vr)
+
+        b_rows = const.tile([P, D], BF16)
+        nc.sync.dma_start(out=b_rows[:], in_=b_g.partition_broadcast(P))
+        bg_rows = const.tile([P, 1], BF16)
+        nc.sync.dma_start(out=bg_rows[:], in_=bg.partition_broadcast(P))
+        bias = const.tile([P, D], F32)
+        nc.vector.tensor_tensor(out=bias[:], in0=b_rows[:], in1=bg_rows[:].to_broadcast([P, D]), op=ALU.add)
+
+        def prepare(rt):
+            c, j = divmod(rt, J)
+            if j == 0:
+                if c > 0:
+                    load_chunk(c)
+                at = psum_t.tile([P, J, P], F32, tag="tp")
+                for jj in range(J):
+                    nc.tensor.transpose(at[:, jj, :], a_tiles[c][:, jj, :].bitcast(F32), ident[:])
+                aT = loads.tile([P, S, J, P], BF16, name="aT")
+                nc.scalar.copy(out=aT[:], in_=at[:].bitcast(BF16).rearrange("n j (b s) -> n s j b", s=S))
+                aT_tiles[c] = aT
+            h_words = h_tiles[c][:, j, :].bitcast(F32)
+            ht = psum_t.tile([P, G, 2, P], F32, tag="tp")
+            for g in range(G):
+                for u in range(2):
+                    nc.tensor.transpose(ht[:, g, u, :], h_words[:, 256 * g + u : 256 * (g + 1) : 2], ident[:])
+            grouped = quant.tile([P, G, P, 2], F32, align_bytes=64)
+            nc.scalar.copy(out=grouped[:], in_=ht[:].rearrange("p g u b -> p g b u"))
+            codes = quant.tile([P, G, P], U32, align_bytes=64)
+            scales = quant.tile([P, G, P], U8, align_bytes=64)
+            nc.vector.quantize_mx(
+                out=codes[:].rearrange("p g b -> p (g b)").bitcast(FP8X4),
+                scales=scales[:].rearrange("p g b -> p (g b)"),
+                in_=grouped[:].rearrange("p g b u -> p (g b u)").bitcast(BF16),
+            )
+            code_tiles[rt], scale_tiles[rt] = codes, scales
+
+        def compute(rt):
+            c, j = divmod(rt, J)
+            codes, scales = code_tiles.pop(rt), scale_tiles.pop(rt)
+            o_sb = work.tile([P, D], F32, name="o_sb")
+            for s in range(S):
+                cols = slice(DS * s, DS * (s + 1))
+                zp = psum_z.tile([P, DS], F32)
+                for g in range(G):
+                    nc.tensor.matmul_mx(
+                        out=zp[:],
+                        lhsT=codes[:, g, :].bitcast(FP8X4),
+                        lhsT_scale=scales[:, g, :],
+                        rhs=w_words[:, g, 2 * DS * s : 2 * DS * (s + 1)].bitcast(FP4X4),
+                        rhs_scale=w_planes[:, g, cols],
+                        start=(g == 0),
+                        stop=(g == G - 1),
+                    )
+                hhp = psum_h.tile([P, DS], F32)
+                nc.tensor.matmul(out=hhp[:], lhsT=aT_tiles[c][:, s, j, :], rhs=vr_sb[:, s, :], start=True, stop=True)
+
+                xb = work.tile([P, DS], F32)
+                nc.gpsimd.tensor_tensor(out=xb[:], in0=x_tiles[c][:, j, cols], in1=bias[:, cols], op=ALU.add)
+                z = work.tile([P, DS], F32)
+                nc.vector.tensor_tensor(out=z[:], in0=zp[:], in1=xb[:], op=ALU.add)
+                keep = work.tile([P, DS], F32)
+                nc.scalar.activation(out=keep[:], in_=z[:], func=ACT.Sigmoid, scale=-1.0)
+                diff = work.tile([P, DS], F32)
+                nc.vector.tensor_tensor(out=diff[:], in0=hhp[:], in1=h_tiles[c][:, j, cols], op=ALU.subtract)
+                back = work.tile([P, DS], F32)
+                nc.vector.tensor_tensor(out=back[:], in0=keep[:], in1=diff[:], op=ALU.mult)
+                nc.vector.tensor_tensor(out=o_sb[:, cols], in0=hhp[:], in1=back[:], op=ALU.subtract)
+            nc.sync.dma_start(out=out_chunks[c][:, j, :], in_=o_sb[:])
+
+        for rt in range(ROW_TILES + AHEAD):
+            if rt < ROW_TILES:
+                prepare(rt)
+            if rt >= AHEAD:
+                compute(rt - AHEAD)

@@ -18,9 +18,13 @@ DS = D // S
 P = 128
 G = D // 512
 J = 4
-CHUNKS = B // (P * J)
-ROW_TILES = CHUNKS * J
-AHEAD = 2
+ROWS = P * J
+CHUNKS = B // ROWS
+BLOCKS = D // P
+PER_CHUNK = J * S
+UNITS = CHUNKS * PER_CHUNK
+GATE_LAG = PER_CHUNK + 1
+BLEND_LAG = 2 * PER_CHUNK + 1
 
 FLOPS = 2 * B * D * D + 2 * B * N * D
 
@@ -34,26 +38,31 @@ def tile_tpru_pb_t_kernel(tc, a, vr, h, x2g, w_g_words, w_g_scales, b_g, bg, out
 
     with ExitStack() as ctx:
         const = ctx.enter_context(tc.tile_pool(name="const", bufs=1))
+        state = ctx.enter_context(tc.tile_pool(name="state", bufs=5))
         loads = ctx.enter_context(tc.tile_pool(name="loads", bufs=3))
-        quant = ctx.enter_context(tc.tile_pool(name="quant", bufs=AHEAD + 2))
+        gates = ctx.enter_context(tc.tile_pool(name="gates", bufs=2))
         work = ctx.enter_context(tc.tile_pool(name="work", bufs=3))
-        psum_t = ctx.enter_context(tc.psum_pool(name="psum_t", bufs=2))
-        psum_z = ctx.enter_context(tc.psum_pool(name="psum_z", bufs=3))
+        psum_t = ctx.enter_context(tc.psum_pool(name="psum_t", bufs=1))
+        psum_g = ctx.enter_context(tc.psum_pool(name="psum_g", bufs=2))
+        psum_z = ctx.enter_context(tc.psum_pool(name="psum_z", bufs=2))
         psum_h = ctx.enter_context(tc.psum_pool(name="psum_h", bufs=3))
+        ctx.enter_context(tc.manual_schedule())
 
-        h_tiles, x_tiles, a_tiles, aT_tiles = {}, {}, {}, {}
-        code_tiles, scale_tiles = {}, {}
+        h_tiles, a_tiles, x_tiles, aT_tiles = {}, {}, {}, {}
+        grouped_tiles, code_tiles, scale_tiles, zT_tiles = {}, {}, {}, {}
+        zb_tiles, hh_tiles, back_tiles, o_tiles = {}, {}, {}, {}
 
-        def load_chunk(c):
-            h_sb = loads.tile([P, J, D], BF16, name="h_sb")
-            nc.sync.dma_start(out=h_sb[:], in_=h_chunks[c])
-            a_sb = loads.tile([P, J, N * S], BF16, name="a_sb")
-            nc.sync.dma_start(out=a_sb[:], in_=a_chunks[c])
-            x_sb = loads.tile([P, J, D], BF16, name="x_sb")
-            nc.sync.dma_start(out=x_sb[:], in_=x_chunks[c])
-            h_tiles[c], a_tiles[c], x_tiles[c] = h_sb, a_sb, x_sb
+        def load_state(c):
+            h_tiles[c] = state.tile([P, J, D], BF16, name="h_sb")
+            nc.sync.dma_start(out=h_tiles[c][:], in_=h_chunks[c])
+            a_tiles[c] = loads.tile([P, J, N * S], BF16, name="a_sb")
+            nc.sync.dma_start(out=a_tiles[c][:], in_=a_chunks[c])
 
-        load_chunk(0)
+        def load_gate_input(c):
+            x_tiles[c] = loads.tile([P, J, D], BF16, name="x_sb")
+            nc.sync.dma_start(out=x_tiles[c][:], in_=x_chunks[c])
+
+        load_state(0)
 
         ident = const.tile([P, P], F32)
         make_identity(nc, ident[:])
@@ -72,75 +81,134 @@ def tile_tpru_pb_t_kernel(tc, a, vr, h, x2g, w_g_words, w_g_scales, b_g, bg, out
         vr_sb = const.tile([P, S, DS], BF16)
         nc.sync.dma_start(out=vr_sb[:], in_=vr)
 
-        b_rows = const.tile([P, D], BF16)
-        nc.sync.dma_start(out=b_rows[:], in_=b_g.partition_broadcast(P))
+        b_rows = const.tile([P, P], BF16)
+        nc.vector.memset(b_rows[:], 0.0)
+        nc.sync.dma_start(out=b_rows[0:BLOCKS, :], in_=b_g.rearrange("(r c) -> r c", c=P))
         bg_rows = const.tile([P, 1], BF16)
         nc.sync.dma_start(out=bg_rows[:], in_=bg.partition_broadcast(P))
-        bias = const.tile([P, D], F32)
-        nc.vector.tensor_tensor(out=bias[:], in0=b_rows[:], in1=bg_rows[:].to_broadcast([P, D]), op=ALU.add)
+        b_rows32 = const.tile([P, P], F32)
+        nc.vector.tensor_copy(out=b_rows32[:], in_=b_rows[:])
+        b_cols = psum_t.tile([P, 3, P], F32, tag="tp")
+        nc.tensor.transpose(b_cols[:, 0, :], b_rows32[:], ident[:])
+        bias_cols = const.tile([P, BLOCKS], F32)
+        nc.vector.tensor_tensor(
+            out=bias_cols[:], in0=b_cols[:, 0, 0:BLOCKS], in1=bg_rows[:].to_broadcast([P, BLOCKS]), op=ALU.add
+        )
 
-        def prepare(rt):
-            c, j = divmod(rt, J)
-            if j == 0:
-                if c > 0:
-                    load_chunk(c)
-                at = psum_t.tile([P, J, P], F32, tag="tp")
-                for jj in range(J):
-                    nc.tensor.transpose(at[:, jj, :], a_tiles[c][:, jj, :].bitcast(F32), ident[:])
-                aT = loads.tile([P, S, J, P], BF16, name="aT")
-                nc.scalar.copy(out=aT[:], in_=at[:].bitcast(BF16).rearrange("n j (b s) -> n s j b", s=S))
-                aT_tiles[c] = aT
+        def transpose_piece(u):
+            c, piece = divmod(u, PER_CHUNK)
+            j, g = divmod(piece, G)
+            tp = psum_t.tile([P, 3, P], F32, tag="tp")
             h_words = h_tiles[c][:, j, :].bitcast(F32)
-            ht = psum_t.tile([P, G, 2, P], F32, tag="tp")
-            for g in range(G):
-                for u in range(2):
-                    nc.tensor.transpose(ht[:, g, u, :], h_words[:, 256 * g + u : 256 * (g + 1) : 2], ident[:])
-            grouped = quant.tile([P, G, P, 2], F32, align_bytes=64)
-            nc.scalar.copy(out=grouped[:], in_=ht[:].rearrange("p g u b -> p g b u"))
-            codes = quant.tile([P, G, P], U32, align_bytes=64)
-            scales = quant.tile([P, G, P], U8, align_bytes=64)
+            for u2 in range(2):
+                nc.tensor.transpose(tp[:, u2, :], h_words[:, 256 * g + u2 : 256 * (g + 1) : 2], ident[:])
+            if g == 0:
+                nc.tensor.transpose(tp[:, 2, :], a_tiles[c][:, j, :].bitcast(F32), ident[:])
+            grouped = work.tile([P, P, 2], F32, name="grouped", align_bytes=64)
+            nc.scalar.copy(out=grouped[:], in_=tp[:, 0:2, :].rearrange("p u b -> p b u"))
+            grouped_tiles[u] = grouped
+            if g == 0:
+                if j == 0:
+                    aT_tiles[c] = state.tile([P, S, J, P], BF16, name="aT")
+                nc.scalar.copy(
+                    out=aT_tiles[c][:, :, j, :], in_=tp[:, 2, :].bitcast(BF16).rearrange("n (b s) -> n s b", s=S)
+                )
+
+        def quantise_piece(u):
+            c, piece = divmod(u, PER_CHUNK)
+            j, g = divmod(piece, G)
+            if piece == 0:
+                code_tiles[c] = loads.tile([P, G, ROWS], U32, name="codes", align_bytes=64)
+                scale_tiles[c] = loads.tile([P, G, ROWS], U8, name="scales", align_bytes=64)
+            rows = slice(P * j, P * (j + 1))
             nc.vector.quantize_mx(
-                out=codes[:].rearrange("p g b -> p (g b)").bitcast(FP8X4),
-                scales=scales[:].rearrange("p g b -> p (g b)"),
-                in_=grouped[:].rearrange("p g b u -> p (g b u)").bitcast(BF16),
+                out=code_tiles[c][:, g, rows].bitcast(FP8X4),
+                scales=scale_tiles[c][:, g, rows],
+                in_=grouped_tiles.pop(u)[:].rearrange("p b u -> p (b u)").bitcast(BF16),
             )
-            code_tiles[rt], scale_tiles[rt] = codes, scales
 
-        def compute(rt):
-            c, j = divmod(rt, J)
-            codes, scales = code_tiles.pop(rt), scale_tiles.pop(rt)
-            o_sb = work.tile([P, D], F32, name="o_sb")
-            for s in range(S):
-                cols = slice(DS * s, DS * (s + 1))
-                zp = psum_z.tile([P, DS], F32)
-                for g in range(G):
-                    nc.tensor.matmul_mx(
-                        out=zp[:],
-                        lhsT=codes[:, g, :].bitcast(FP8X4),
-                        lhsT_scale=scales[:, g, :],
-                        rhs=w_words[:, g, 2 * DS * s : 2 * DS * (s + 1)].bitcast(FP4X4),
-                        rhs_scale=w_planes[:, g, cols],
-                        start=(g == 0),
-                        stop=(g == G - 1),
-                    )
-                hhp = psum_h.tile([P, DS], F32)
-                nc.tensor.matmul(out=hhp[:], lhsT=aT_tiles[c][:, s, j, :], rhs=vr_sb[:, s, :], start=True, stop=True)
+        def gate_block(u):
+            c, block = divmod(u, PER_CHUNK)
+            gt = psum_g.tile([P, ROWS], F32)
+            for g in range(G):
+                nc.tensor.matmul_mx(
+                    out=gt[:],
+                    lhsT=w_words[:, g, 2 * P * block : 2 * P * (block + 1)].bitcast(FP4X4),
+                    lhsT_scale=w_planes[:, g, P * block : P * (block + 1)],
+                    rhs=code_tiles[c][:, g, :].bitcast(FP8X4),
+                    rhs_scale=scale_tiles[c][:, g, :],
+                    start=(g == 0),
+                    stop=(g == G - 1),
+                )
+            if block == 0:
+                zT_tiles[c] = gates.tile([P, BLOCKS, ROWS], F32, name="zT")
+            nc.scalar.activation(
+                out=zT_tiles[c][:, block, :], in_=gt[:], func=ACT.Identity, bias=bias_cols[:, block : block + 1]
+            )
 
-                xb = work.tile([P, DS], F32)
-                nc.gpsimd.tensor_tensor(out=xb[:], in0=x_tiles[c][:, j, cols], in1=bias[:, cols], op=ALU.add)
-                z = work.tile([P, DS], F32)
-                nc.vector.tensor_tensor(out=z[:], in0=zp[:], in1=xb[:], op=ALU.add)
-                keep = work.tile([P, DS], F32)
-                nc.scalar.activation(out=keep[:], in_=z[:], func=ACT.Sigmoid, scale=-1.0)
-                diff = work.tile([P, DS], F32)
-                nc.vector.tensor_tensor(out=diff[:], in0=hhp[:], in1=h_tiles[c][:, j, cols], op=ALU.subtract)
-                back = work.tile([P, DS], F32)
-                nc.vector.tensor_tensor(out=back[:], in0=keep[:], in1=diff[:], op=ALU.mult)
-                nc.vector.tensor_tensor(out=o_sb[:, cols], in0=hhp[:], in1=back[:], op=ALU.subtract)
-            nc.sync.dma_start(out=out_chunks[c][:, j, :], in_=o_sb[:])
+        def turn_gate_back(u):
+            c, unit = divmod(u, PER_CHUNK)
+            j, s = divmod(unit, S)
+            zb = psum_z.tile([P, DS], F32)
+            for q in range(DS // P):
+                nc.tensor.transpose(
+                    zb[:, P * q : P * (q + 1)], zT_tiles[c][:, (DS // P) * s + q, P * j : P * (j + 1)], ident[:]
+                )
+            zb_tiles[u] = zb
 
-        for rt in range(ROW_TILES + AHEAD):
-            if rt < ROW_TILES:
-                prepare(rt)
-            if rt >= AHEAD:
-                compute(rt - AHEAD)
+        def role_matmul(u):
+            c, unit = divmod(u, PER_CHUNK)
+            j, s = divmod(unit, S)
+            hhp = psum_h.tile([P, DS], F32)
+            nc.tensor.matmul(out=hhp[:], lhsT=aT_tiles[c][:, s, j, :], rhs=vr_sb[:, s, :], start=True, stop=True)
+            hh_tiles[u] = hhp
+
+        def gate_and_difference(u):
+            c, unit = divmod(u, PER_CHUNK)
+            j, s = divmod(unit, S)
+            cols = slice(DS * s, DS * (s + 1))
+            z = work.tile([P, DS], F32)
+            nc.vector.tensor_tensor(out=z[:], in0=zb_tiles.pop(u)[:], in1=x_tiles[c][:, j, cols], op=ALU.add)
+            keep = work.tile([P, DS], F32)
+            nc.scalar.activation(out=keep[:], in_=z[:], func=ACT.Sigmoid, scale=-1.0)
+            diff = work.tile([P, DS], F32)
+            nc.vector.tensor_tensor(out=diff[:], in0=hh_tiles[u][:], in1=h_tiles[c][:, j, cols], op=ALU.subtract)
+            back = work.tile([P, DS], F32)
+            nc.gpsimd.tensor_tensor(out=back[:], in0=keep[:], in1=diff[:], op=ALU.mult)
+            back_tiles[u] = back
+
+        def finish(u):
+            c, unit = divmod(u, PER_CHUNK)
+            j, s = divmod(unit, S)
+            if s == 0:
+                o_tiles[(c, j)] = work.tile([P, D], F32, name="o_sb")
+            o_sb = o_tiles[(c, j)]
+            nc.vector.tensor_tensor(
+                out=o_sb[:, DS * s : DS * (s + 1)], in0=hh_tiles.pop(u)[:], in1=back_tiles.pop(u)[:], op=ALU.subtract
+            )
+            if s == S - 1:
+                nc.sync.dma_start(out=out_chunks[c][:, j, :], in_=o_sb[:])
+
+        for step in range(UNITS + BLEND_LAG + 1):
+            gate_unit = step - GATE_LAG
+            blend_unit = step - BLEND_LAG
+            if step % PER_CHUNK == 0:
+                ahead = step // PER_CHUNK + 1
+                if ahead < CHUNKS:
+                    load_state(ahead)
+                if 0 <= ahead - 2 < CHUNKS:
+                    load_gate_input(ahead - 2)
+            if 0 <= blend_unit < UNITS:
+                turn_gate_back(blend_unit)
+            if step < UNITS:
+                transpose_piece(step)
+            if 0 <= blend_unit < UNITS:
+                role_matmul(blend_unit)
+            if 0 <= gate_unit < UNITS:
+                gate_block(gate_unit)
+            if 0 <= blend_unit < UNITS:
+                gate_and_difference(blend_unit)
+            if 0 <= blend_unit - 1 < UNITS:
+                finish(blend_unit - 1)
+            if step < UNITS:
+                quantise_piece(step)

@@ -18,13 +18,9 @@ DS = D // S
 P = 128
 G = D // 512
 J = 4
-ROWS = P * J
-CHUNKS = B // ROWS
-BLOCKS = D // P
-PER_CHUNK = J * S
-UNITS = CHUNKS * PER_CHUNK
-GATE_LAG = PER_CHUNK + 1
-BLEND_LAG = 2 * PER_CHUNK + 1
+CHUNKS = B // (P * J)
+ROW_TILES = CHUNKS * J
+AHEAD = 2
 
 FLOPS = 2 * B * D * D + 2 * B * N * D
 
@@ -38,31 +34,26 @@ def tile_tpru_pb_t_kernel(tc, a, vr, h, x2g, w_g_words, w_g_scales, b_g, bg, out
 
     with ExitStack() as ctx:
         const = ctx.enter_context(tc.tile_pool(name="const", bufs=1))
-        state = ctx.enter_context(tc.tile_pool(name="state", bufs=5))
         loads = ctx.enter_context(tc.tile_pool(name="loads", bufs=3))
-        gates = ctx.enter_context(tc.tile_pool(name="gates", bufs=2))
+        quant = ctx.enter_context(tc.tile_pool(name="quant", bufs=AHEAD + 2))
         work = ctx.enter_context(tc.tile_pool(name="work", bufs=3))
-        psum_t = ctx.enter_context(tc.psum_pool(name="psum_t", bufs=1))
-        psum_g = ctx.enter_context(tc.psum_pool(name="psum_g", bufs=2))
+        psum_t = ctx.enter_context(tc.psum_pool(name="psum_t", bufs=2))
         psum_z = ctx.enter_context(tc.psum_pool(name="psum_z", bufs=2))
-        psum_h = ctx.enter_context(tc.psum_pool(name="psum_h", bufs=3))
-        ctx.enter_context(tc.manual_schedule())
+        psum_h = ctx.enter_context(tc.psum_pool(name="psum_h", bufs=4))
 
-        h_tiles, a_tiles, x_tiles, aT_tiles = {}, {}, {}, {}
-        grouped_tiles, code_tiles, scale_tiles, zT_tiles = {}, {}, {}, {}
-        zb_tiles, hh_tiles, back_tiles, o_tiles = {}, {}, {}, {}
+        h_tiles, x_tiles, a_tiles, aT_tiles = {}, {}, {}, {}
+        code_tiles, scale_tiles, xb_tiles = {}, {}, {}
 
-        def load_state(c):
-            h_tiles[c] = state.tile([P, J, D], BF16, name="h_sb")
-            nc.sync.dma_start(out=h_tiles[c][:], in_=h_chunks[c])
-            a_tiles[c] = loads.tile([P, J, N * S], BF16, name="a_sb")
-            nc.sync.dma_start(out=a_tiles[c][:], in_=a_chunks[c])
+        def load_chunk(c):
+            h_sb = loads.tile([P, J, D], BF16, name="h_sb")
+            nc.sync.dma_start(out=h_sb[:], in_=h_chunks[c])
+            a_sb = loads.tile([P, J, N * S], BF16, name="a_sb")
+            nc.sync.dma_start(out=a_sb[:], in_=a_chunks[c])
+            x_sb = loads.tile([P, J, D], BF16, name="x_sb")
+            nc.sync.dma_start(out=x_sb[:], in_=x_chunks[c])
+            h_tiles[c], a_tiles[c], x_tiles[c] = h_sb, a_sb, x_sb
 
-        def load_gate_input(c):
-            x_tiles[c] = loads.tile([P, J, D], BF16, name="x_sb")
-            nc.sync.dma_start(out=x_tiles[c][:], in_=x_chunks[c])
-
-        load_state(0)
+        load_chunk(0)
 
         ident = const.tile([P, P], F32)
         make_identity(nc, ident[:])
@@ -81,134 +72,79 @@ def tile_tpru_pb_t_kernel(tc, a, vr, h, x2g, w_g_words, w_g_scales, b_g, bg, out
         vr_sb = const.tile([P, S, DS], BF16)
         nc.sync.dma_start(out=vr_sb[:], in_=vr)
 
-        b_rows = const.tile([P, P], BF16)
-        nc.vector.memset(b_rows[:], 0.0)
-        nc.sync.dma_start(out=b_rows[0:BLOCKS, :], in_=b_g.rearrange("(r c) -> r c", c=P))
+        b_rows = const.tile([P, D], BF16)
+        nc.sync.dma_start(out=b_rows[:], in_=b_g.partition_broadcast(P))
         bg_rows = const.tile([P, 1], BF16)
         nc.sync.dma_start(out=bg_rows[:], in_=bg.partition_broadcast(P))
-        b_rows32 = const.tile([P, P], F32)
-        nc.vector.tensor_copy(out=b_rows32[:], in_=b_rows[:])
-        b_cols = psum_t.tile([P, 3, P], F32, tag="tp")
-        nc.tensor.transpose(b_cols[:, 0, :], b_rows32[:], ident[:])
-        bias_cols = const.tile([P, BLOCKS], F32)
-        nc.vector.tensor_tensor(
-            out=bias_cols[:], in0=b_cols[:, 0, 0:BLOCKS], in1=bg_rows[:].to_broadcast([P, BLOCKS]), op=ALU.add
-        )
+        bias = const.tile([P, D], F32)
+        nc.vector.tensor_tensor(out=bias[:], in0=b_rows[:], in1=bg_rows[:].to_broadcast([P, D]), op=ALU.add)
 
-        def transpose_piece(u):
-            c, piece = divmod(u, PER_CHUNK)
-            j, g = divmod(piece, G)
-            tp = psum_t.tile([P, 3, P], F32, tag="tp")
+        def prepare(rt):
+            c, j = divmod(rt, J)
+            if j == 0:
+                if c > 0:
+                    load_chunk(c)
+                at = psum_t.tile([P, J, P], F32, tag="tp")
+                for jj in range(J):
+                    nc.tensor.transpose(at[:, jj, :], a_tiles[c][:, jj, :].bitcast(F32), ident[:])
+                aT = loads.tile([P, S, J, P], BF16, name="aT")
+                nc.scalar.copy(out=aT[:], in_=at[:].bitcast(BF16).rearrange("n j (b s) -> n s j b", s=S))
+                aT_tiles[c] = aT
             h_words = h_tiles[c][:, j, :].bitcast(F32)
-            for u2 in range(2):
-                nc.tensor.transpose(tp[:, u2, :], h_words[:, 256 * g + u2 : 256 * (g + 1) : 2], ident[:])
-            if g == 0:
-                nc.tensor.transpose(tp[:, 2, :], a_tiles[c][:, j, :].bitcast(F32), ident[:])
-            grouped = work.tile([P, P, 2], F32, name="grouped", align_bytes=64)
-            nc.scalar.copy(out=grouped[:], in_=tp[:, 0:2, :].rearrange("p u b -> p b u"))
-            grouped_tiles[u] = grouped
-            if g == 0:
-                if j == 0:
-                    aT_tiles[c] = state.tile([P, S, J, P], BF16, name="aT")
-                nc.scalar.copy(
-                    out=aT_tiles[c][:, :, j, :], in_=tp[:, 2, :].bitcast(BF16).rearrange("n (b s) -> n s b", s=S)
-                )
-
-        def quantise_piece(u):
-            c, piece = divmod(u, PER_CHUNK)
-            j, g = divmod(piece, G)
-            if piece == 0:
-                code_tiles[c] = loads.tile([P, G, ROWS], U32, name="codes", align_bytes=64)
-                scale_tiles[c] = loads.tile([P, G, ROWS], U8, name="scales", align_bytes=64)
-            rows = slice(P * j, P * (j + 1))
-            nc.vector.quantize_mx(
-                out=code_tiles[c][:, g, rows].bitcast(FP8X4),
-                scales=scale_tiles[c][:, g, rows],
-                in_=grouped_tiles.pop(u)[:].rearrange("p b u -> p (b u)").bitcast(BF16),
-            )
-
-        def gate_block(u):
-            c, block = divmod(u, PER_CHUNK)
-            gt = psum_g.tile([P, ROWS], F32)
+            ht = psum_t.tile([P, G, 2, P], F32, tag="tp")
             for g in range(G):
-                nc.tensor.matmul_mx(
-                    out=gt[:],
-                    lhsT=w_words[:, g, 2 * P * block : 2 * P * (block + 1)].bitcast(FP4X4),
-                    lhsT_scale=w_planes[:, g, P * block : P * (block + 1)],
-                    rhs=code_tiles[c][:, g, :].bitcast(FP8X4),
-                    rhs_scale=scale_tiles[c][:, g, :],
-                    start=(g == 0),
-                    stop=(g == G - 1),
-                )
-            if block == 0:
-                zT_tiles[c] = gates.tile([P, BLOCKS, ROWS], F32, name="zT")
-            nc.scalar.activation(
-                out=zT_tiles[c][:, block, :], in_=gt[:], func=ACT.Identity, bias=bias_cols[:, block : block + 1]
+                for u in range(2):
+                    nc.tensor.transpose(ht[:, g, u, :], h_words[:, 256 * g + u : 256 * (g + 1) : 2], ident[:])
+            grouped = quant.tile([P, G, P, 2], F32, align_bytes=64)
+            nc.scalar.copy(out=grouped[:], in_=ht[:].rearrange("p g u b -> p g b u"))
+            codes = quant.tile([P, G, P], U32, align_bytes=64)
+            scales = quant.tile([P, G, P], U8, align_bytes=64)
+            nc.vector.quantize_mx(
+                out=codes[:].rearrange("p g b -> p (g b)").bitcast(FP8X4),
+                scales=scales[:].rearrange("p g b -> p (g b)"),
+                in_=grouped[:].rearrange("p g b u -> p (g b u)").bitcast(BF16),
             )
+            code_tiles[rt], scale_tiles[rt] = codes, scales
+            xb = quant.tile([P, D], F32)
+            nc.gpsimd.tensor_tensor(out=xb[:], in0=x_tiles[c][:, j, :], in1=bias[:], op=ALU.add)
+            xb_tiles[rt] = xb
 
-        def turn_gate_back(u):
-            c, unit = divmod(u, PER_CHUNK)
-            j, s = divmod(unit, S)
-            zb = psum_z.tile([P, DS], F32)
-            for q in range(DS // P):
-                nc.tensor.transpose(
-                    zb[:, P * q : P * (q + 1)], zT_tiles[c][:, (DS // P) * s + q, P * j : P * (j + 1)], ident[:]
-                )
-            zb_tiles[u] = zb
-
-        def role_matmul(u):
-            c, unit = divmod(u, PER_CHUNK)
-            j, s = divmod(unit, S)
-            hhp = psum_h.tile([P, DS], F32)
-            nc.tensor.matmul(out=hhp[:], lhsT=aT_tiles[c][:, s, j, :], rhs=vr_sb[:, s, :], start=True, stop=True)
-            hh_tiles[u] = hhp
-
-        def gate_and_difference(u):
-            c, unit = divmod(u, PER_CHUNK)
-            j, s = divmod(unit, S)
-            cols = slice(DS * s, DS * (s + 1))
-            z = work.tile([P, DS], F32)
-            nc.vector.tensor_tensor(out=z[:], in0=zb_tiles.pop(u)[:], in1=x_tiles[c][:, j, cols], op=ALU.add)
-            keep = work.tile([P, DS], F32)
+        def compute(rt):
+            c, j = divmod(rt, J)
+            codes, scales, xb = code_tiles.pop(rt), scale_tiles.pop(rt), xb_tiles.pop(rt)
+            z = work.tile([P, D], F32)
+            diff = work.tile([P, D], F32)
+            hh_banks = []
+            for s in range(S):
+                cols = slice(DS * s, DS * (s + 1))
+                zp = psum_z.tile([P, DS], F32)
+                for g in range(G):
+                    nc.tensor.matmul_mx(
+                        out=zp[:],
+                        lhsT=codes[:, g, :].bitcast(FP8X4),
+                        lhsT_scale=scales[:, g, :],
+                        rhs=w_words[:, g, 2 * DS * s : 2 * DS * (s + 1)].bitcast(FP4X4),
+                        rhs_scale=w_planes[:, g, cols],
+                        start=(g == 0),
+                        stop=(g == G - 1),
+                    )
+                hhp = psum_h.tile([P, DS], F32)
+                nc.tensor.matmul(out=hhp[:], lhsT=aT_tiles[c][:, s, j, :], rhs=vr_sb[:, s, :], start=True, stop=True)
+                hh_banks.append(hhp)
+                nc.vector.tensor_tensor(out=z[:, cols], in0=zp[:], in1=xb[:, cols], op=ALU.add)
+                nc.vector.tensor_tensor(out=diff[:, cols], in0=hhp[:], in1=h_tiles[c][:, j, cols], op=ALU.subtract)
+            keep = work.tile([P, D], F32)
             nc.scalar.activation(out=keep[:], in_=z[:], func=ACT.Sigmoid, scale=-1.0)
-            diff = work.tile([P, DS], F32)
-            nc.vector.tensor_tensor(out=diff[:], in0=hh_tiles[u][:], in1=h_tiles[c][:, j, cols], op=ALU.subtract)
-            back = work.tile([P, DS], F32)
+            back = work.tile([P, D], F32)
             nc.gpsimd.tensor_tensor(out=back[:], in0=keep[:], in1=diff[:], op=ALU.mult)
-            back_tiles[u] = back
+            o_sb = work.tile([P, D], F32)
+            for s in range(S):
+                cols = slice(DS * s, DS * (s + 1))
+                nc.vector.tensor_tensor(out=o_sb[:, cols], in0=hh_banks[s][:], in1=back[:, cols], op=ALU.subtract)
+            nc.sync.dma_start(out=out_chunks[c][:, j, :], in_=o_sb[:])
 
-        def finish(u):
-            c, unit = divmod(u, PER_CHUNK)
-            j, s = divmod(unit, S)
-            if s == 0:
-                o_tiles[(c, j)] = work.tile([P, D], F32, name="o_sb")
-            o_sb = o_tiles[(c, j)]
-            nc.vector.tensor_tensor(
-                out=o_sb[:, DS * s : DS * (s + 1)], in0=hh_tiles.pop(u)[:], in1=back_tiles.pop(u)[:], op=ALU.subtract
-            )
-            if s == S - 1:
-                nc.sync.dma_start(out=out_chunks[c][:, j, :], in_=o_sb[:])
-
-        for step in range(UNITS + BLEND_LAG + 1):
-            gate_unit = step - GATE_LAG
-            blend_unit = step - BLEND_LAG
-            if step % PER_CHUNK == 0:
-                ahead = step // PER_CHUNK + 1
-                if ahead < CHUNKS:
-                    load_state(ahead)
-                if 0 <= ahead - 2 < CHUNKS:
-                    load_gate_input(ahead - 2)
-            if 0 <= blend_unit < UNITS:
-                turn_gate_back(blend_unit)
-            if step < UNITS:
-                transpose_piece(step)
-            if 0 <= blend_unit < UNITS:
-                role_matmul(blend_unit)
-            if 0 <= gate_unit < UNITS:
-                gate_block(gate_unit)
-            if 0 <= blend_unit < UNITS:
-                gate_and_difference(blend_unit)
-            if 0 <= blend_unit - 1 < UNITS:
-                finish(blend_unit - 1)
-            if step < UNITS:
-                quantise_piece(step)
+        for rt in range(ROW_TILES + AHEAD):
+            if rt < ROW_TILES:
+                prepare(rt)
+            if rt >= AHEAD:
+                compute(rt - AHEAD)

@@ -27,10 +27,10 @@ FLOPS = 2 * B * D * D + 2 * B * N * D
 
 def tile_tpru_pb_t_kernel(tc, a, vr, h, x2g, w_g_words, w_g_scales, b_g, bg, out):
     nc = tc.nc
-    h_chunks = h.rearrange("(c p j) k -> c p j k", p=P, j=J)
-    x_chunks = x2g.rearrange("(c p j) k -> c p j k", p=P, j=J)
-    a_chunks = a.rearrange("(c p j) n s -> c p j (n s)", p=P, j=J)
-    out_chunks = out.rearrange("(c p j) k -> c p j k", p=P, j=J)
+    h_chunks = h.rearrange("(c j p) k -> c p j k", p=P, j=J)
+    x_chunks = x2g.rearrange("(c j p) k -> c p j k", p=P, j=J)
+    a_chunks = a.rearrange("(c j p) n s -> c p j (n s)", p=P, j=J)
+    out_chunks = out.rearrange("(c j p) k -> c p j k", p=P, j=J)
 
     with ExitStack() as ctx:
         const = ctx.enter_context(tc.tile_pool(name="const", bufs=1))

@@ -20,7 +20,6 @@ G = D // 512
 J = 4
 CHUNKS = B // (P * J)
 ROW_TILES = CHUNKS * J
-AHEAD = 2
 
 FLOPS = 2 * B * D * D + 2 * B * N * D
 
@@ -30,28 +29,30 @@ def tile_tpru_pb_t_kernel(tc, a, vr, h, x2g, w_g_words, w_g_scales, b_g, bg, out
     h_chunks = h.rearrange("(c j p) k -> c p j k", p=P, j=J)
     x_chunks = x2g.rearrange("(c j p) k -> c p j k", p=P, j=J)
     a_chunks = a.rearrange("(c j p) n s -> c p j (n s)", p=P, j=J)
-    out_chunks = out.rearrange("(c j p) k -> c p j k", p=P, j=J)
+    out_tiles = out.rearrange("(r p) k -> r p k", p=P)
+    first, second = slice(0, DS), slice(DS, D)
 
     with ExitStack() as ctx:
         const = ctx.enter_context(tc.tile_pool(name="const", bufs=1))
-        loads = ctx.enter_context(tc.tile_pool(name="loads", bufs=3))
-        quant = ctx.enter_context(tc.tile_pool(name="quant", bufs=AHEAD + 2))
+        loads = ctx.enter_context(tc.tile_pool(name="loads", bufs=4))
+        quant = ctx.enter_context(tc.tile_pool(name="quant", bufs=4))
         work = ctx.enter_context(tc.tile_pool(name="work", bufs=3))
         psum_t = ctx.enter_context(tc.psum_pool(name="psum_t", bufs=2))
         psum_z = ctx.enter_context(tc.psum_pool(name="psum_z", bufs=2))
         psum_h = ctx.enter_context(tc.psum_pool(name="psum_h", bufs=4))
+        ctx.enter_context(tc.manual_schedule())
 
         h_tiles, x_tiles, a_tiles, aT_tiles = {}, {}, {}, {}
-        code_tiles, scale_tiles, xb_tiles = {}, {}, {}
+        grouped_tiles, code_tiles, scale_tiles, xb_tiles = {}, {}, {}, {}
+        zp_tiles, diff0_tiles, hh1_tiles, gate_tiles, back1_tiles = {}, {}, {}, {}, {}
 
         def load_chunk(c):
-            h_sb = loads.tile([P, J, D], BF16, name="h_sb")
-            nc.sync.dma_start(out=h_sb[:], in_=h_chunks[c])
-            a_sb = loads.tile([P, J, N * S], BF16, name="a_sb")
-            nc.sync.dma_start(out=a_sb[:], in_=a_chunks[c])
-            x_sb = loads.tile([P, J, D], BF16, name="x_sb")
-            nc.sync.dma_start(out=x_sb[:], in_=x_chunks[c])
-            h_tiles[c], a_tiles[c], x_tiles[c] = h_sb, a_sb, x_sb
+            h_tiles[c] = loads.tile([P, J, D], BF16, name="h_sb")
+            nc.sync.dma_start(out=h_tiles[c][:], in_=h_chunks[c])
+            a_tiles[c] = loads.tile([P, J, N * S], BF16, name="a_sb")
+            nc.sync.dma_start(out=a_tiles[c][:], in_=a_chunks[c])
+            x_tiles[c] = loads.tile([P, J, D], BF16, name="x_sb")
+            nc.sync.dma_start(out=x_tiles[c][:], in_=x_chunks[c])
 
         load_chunk(0)
 
@@ -69,6 +70,10 @@ def tile_tpru_pb_t_kernel(tc, a, vr, h, x2g, w_g_words, w_g_scales, b_g, bg, out
                 out=w_planes[32 * quad : 32 * quad + 4].bitcast(I32),
                 in_=w_g_scales[:, 4 * quad : 4 * quad + 4, :].rearrange("g r n -> r g n").bitcast(I32),
             )
+        ident_bf = const.tile([P, P], BF16)
+        make_identity(nc, ident_bf[:])
+        minus_ident = const.tile([P, P], BF16)
+        nc.vector.tensor_scalar_mul(out=minus_ident[:], in0=ident_bf[:], scalar1=-1.0)
         vr_sb = const.tile([P, S, DS], BF16)
         nc.sync.dma_start(out=vr_sb[:], in_=vr)
 
@@ -79,72 +84,95 @@ def tile_tpru_pb_t_kernel(tc, a, vr, h, x2g, w_g_words, w_g_scales, b_g, bg, out
         bias = const.tile([P, D], F32)
         nc.vector.tensor_tensor(out=bias[:], in0=b_rows[:], in1=bg_rows[:].to_broadcast([P, D]), op=ALU.add)
 
-        def prepare(rt):
-            c, j = divmod(rt, J)
+        def transpose(r):
+            c, j = divmod(r, J)
             if j == 0:
-                if c > 0:
-                    load_chunk(c)
+                if c + 1 < CHUNKS:
+                    load_chunk(c + 1)
                 at = psum_t.tile([P, J, P], F32, tag="tp")
                 for jj in range(J):
                     nc.tensor.transpose(at[:, jj, :], a_tiles[c][:, jj, :].bitcast(F32), ident[:])
-                aT = loads.tile([P, S, J, P], BF16, name="aT")
-                nc.scalar.copy(out=aT[:], in_=at[:].bitcast(BF16).rearrange("n j (b s) -> n s j b", s=S))
-                aT_tiles[c] = aT
+                aT_tiles[c] = loads.tile([P, S, J, P], BF16, name="aT")
+                nc.scalar.copy(out=aT_tiles[c][:], in_=at[:].bitcast(BF16).rearrange("n j (b s) -> n s j b", s=S))
             h_words = h_tiles[c][:, j, :].bitcast(F32)
             ht = psum_t.tile([P, G, 2, P], F32, tag="tp")
             for g in range(G):
                 for u in range(2):
                     nc.tensor.transpose(ht[:, g, u, :], h_words[:, 256 * g + u : 256 * (g + 1) : 2], ident[:])
-            grouped = quant.tile([P, G, P, 2], F32, align_bytes=64)
-            nc.scalar.copy(out=grouped[:], in_=ht[:].rearrange("p g u b -> p g b u"))
-            codes = quant.tile([P, G, P], U32, align_bytes=64)
-            scales = quant.tile([P, G, P], U8, align_bytes=64)
-            nc.vector.quantize_mx(
-                out=codes[:].rearrange("p g b -> p (g b)").bitcast(FP8X4),
-                scales=scales[:].rearrange("p g b -> p (g b)"),
-                in_=grouped[:].rearrange("p g b u -> p (g b u)").bitcast(BF16),
-            )
-            code_tiles[rt], scale_tiles[rt] = codes, scales
-            xb = quant.tile([P, D], F32)
-            nc.gpsimd.tensor_tensor(out=xb[:], in0=x_tiles[c][:, j, :], in1=bias[:], op=ALU.add)
-            xb_tiles[rt] = xb
+            grouped_tiles[r] = quant.tile([P, G, P, 2], F32, name="grouped", align_bytes=64)
+            nc.scalar.copy(out=grouped_tiles[r][:], in_=ht[:].rearrange("p g u b -> p g b u"))
 
-        def compute(rt):
-            c, j = divmod(rt, J)
-            codes, scales, xb = code_tiles.pop(rt), scale_tiles.pop(rt), xb_tiles.pop(rt)
-            z = work.tile([P, D], F32)
-            diff = work.tile([P, D], F32)
-            hh_banks = []
+        def quantise(r):
+            c, j = divmod(r, J)
+            code_tiles[r] = quant.tile([P, G, P], U32, name="codes", align_bytes=64)
+            scale_tiles[r] = quant.tile([P, G, P], U8, name="scales", align_bytes=64)
+            nc.vector.quantize_mx(
+                out=code_tiles[r][:].rearrange("p g b -> p (g b)").bitcast(FP8X4),
+                scales=scale_tiles[r][:].rearrange("p g b -> p (g b)"),
+                in_=grouped_tiles.pop(r)[:].rearrange("p g b u -> p (g b u)").bitcast(BF16),
+            )
+            xb_tiles[r] = quant.tile([P, D], F32, name="xb")
+            nc.gpsimd.tensor_tensor(out=xb_tiles[r][:], in0=x_tiles[c][:, j, :], in1=bias[:], op=ALU.add)
+
+        def gate_matmuls(r):
+            codes, scales = code_tiles.pop(r), scale_tiles.pop(r)
             for s in range(S):
-                cols = slice(DS * s, DS * (s + 1))
-                zp = psum_z.tile([P, DS], F32)
+                zp = psum_z.tile([P, DS], F32, name="zp")
                 for g in range(G):
                     nc.tensor.matmul_mx(
                         out=zp[:],
                         lhsT=codes[:, g, :].bitcast(FP8X4),
                         lhsT_scale=scales[:, g, :],
                         rhs=w_words[:, g, 2 * DS * s : 2 * DS * (s + 1)].bitcast(FP4X4),
-                        rhs_scale=w_planes[:, g, cols],
+                        rhs_scale=w_planes[:, g, DS * s : DS * (s + 1)],
                         start=(g == 0),
                         stop=(g == G - 1),
                     )
-                hhp = psum_h.tile([P, DS], F32)
-                nc.tensor.matmul(out=hhp[:], lhsT=aT_tiles[c][:, s, j, :], rhs=vr_sb[:, s, :], start=True, stop=True)
-                hh_banks.append(hhp)
-                nc.vector.tensor_tensor(out=z[:, cols], in0=zp[:], in1=xb[:, cols], op=ALU.add)
-                nc.vector.tensor_tensor(out=diff[:, cols], in0=hhp[:], in1=h_tiles[c][:, j, cols], op=ALU.subtract)
-            keep = work.tile([P, D], F32)
-            nc.scalar.activation(out=keep[:], in_=z[:], func=ACT.Sigmoid, scale=-1.0)
-            back = work.tile([P, D], F32)
-            nc.gpsimd.tensor_tensor(out=back[:], in0=keep[:], in1=diff[:], op=ALU.mult)
-            o_sb = work.tile([P, D], F32)
-            for s in range(S):
-                cols = slice(DS * s, DS * (s + 1))
-                nc.vector.tensor_tensor(out=o_sb[:, cols], in0=hh_banks[s][:], in1=back[:, cols], op=ALU.subtract)
-            nc.sync.dma_start(out=out_chunks[c][:, j, :], in_=o_sb[:])
+                zp_tiles[(r, s)] = zp
 
-        for rt in range(ROW_TILES + AHEAD):
-            if rt < ROW_TILES:
-                prepare(rt)
-            if rt >= AHEAD:
-                compute(rt - AHEAD)
+        def role_matmuls(r):
+            c, j = divmod(r, J)
+            diff0 = psum_h.tile([P, DS], F32, tag="hh")
+            nc.tensor.matmul(out=diff0[:], lhsT=aT_tiles[c][:, 0, j, :], rhs=vr_sb[:, 0, :], start=True, stop=False)
+            nc.tensor.matmul(out=diff0[:], lhsT=minus_ident[:], rhs=h_tiles[c][:, j, first], start=False, stop=True)
+            hh1 = psum_h.tile([P, DS], F32, tag="hh")
+            nc.tensor.matmul(out=hh1[:], lhsT=aT_tiles[c][:, 1, j, :], rhs=vr_sb[:, 1, :], start=True, stop=True)
+            diff0_tiles[r], hh1_tiles[r] = diff0, hh1
+
+        def gate(r):
+            c, j = divmod(r, J)
+            xb = xb_tiles.pop(r)
+            z = work.tile([P, D], F32, name="z")
+            g_sb = work.tile([P, D], F32, name="g_sb")
+            nc.vector.tensor_tensor(out=z[:, first], in0=zp_tiles.pop((r, 0))[:], in1=xb[:, first], op=ALU.add)
+            nc.scalar.activation(out=g_sb[:, first], in_=z[:, first], func=ACT.Sigmoid)
+            nc.vector.tensor_tensor(out=z[:, second], in0=zp_tiles.pop((r, 1))[:], in1=xb[:, second], op=ALU.add)
+            nc.scalar.activation(out=g_sb[:, second], in_=z[:, second], func=ACT.Sigmoid, scale=-1.0)
+            diff1 = work.tile([P, DS], F32, name="diff1")
+            nc.vector.tensor_tensor(out=diff1[:], in0=hh1_tiles[r][:], in1=h_tiles[c][:, j, second], op=ALU.subtract)
+            back1 = work.tile([P, DS], F32, name="back1")
+            nc.gpsimd.tensor_tensor(out=back1[:], in0=g_sb[:, second], in1=diff1[:], op=ALU.mult)
+            gate_tiles[r], back1_tiles[r] = g_sb, back1
+
+        def blend(r):
+            c, j = divmod(r, J)
+            o_sb = work.tile([P, D], F32, name="o_sb")
+            move0 = work.tile([P, DS], F32, name="move0")
+            nc.vector.tensor_tensor(out=move0[:], in0=diff0_tiles.pop(r)[:], in1=gate_tiles.pop(r)[:, first], op=ALU.mult)
+            nc.vector.tensor_tensor(out=o_sb[:, first], in0=move0[:], in1=h_tiles[c][:, j, first], op=ALU.add)
+            nc.vector.tensor_tensor(out=o_sb[:, second], in0=hh1_tiles.pop(r)[:], in1=back1_tiles.pop(r)[:], op=ALU.subtract)
+            nc.sync.dma_start(out=out_tiles[r], in_=o_sb[:])
+
+        for r in range(-3, ROW_TILES + 1):
+            if 0 <= r < ROW_TILES:
+                gate(r)
+            if 0 <= r - 1:
+                blend(r - 1)
+            if 0 <= r + 2 < ROW_TILES:
+                quantise(r + 2)
+            if 0 <= r + 1 < ROW_TILES:
+                gate_matmuls(r + 1)
+            if r + 3 < ROW_TILES:
+                transpose(r + 3)
+            if 0 <= r + 1 < ROW_TILES:
+                role_matmuls(r + 1)

@@ -18,8 +18,14 @@ DS = D // S
 P = 128
 G = D // 512
 J = 4
-CHUNKS = B // (P * J)
-ROW_TILES = CHUNKS * J
+ROWS = P * J
+CHUNKS = B // ROWS
+ROW_TILES = B // P
+BLOCKS = D // P
+BLOCKS_A_TURN = BLOCKS // J
+TRANSPOSE_AHEAD = 10
+QUANTISE_AHEAD = 9
+MATMUL_AHEAD = 5
 
 FLOPS = 2 * B * D * D + 2 * B * N * D
 
@@ -34,30 +40,39 @@ def tile_tpru_pb_t_kernel(tc, a, vr, h, x2g, w_g_words, w_g_scales, b_g, bg, out
 
     with ExitStack() as ctx:
         const = ctx.enter_context(tc.tile_pool(name="const", bufs=1))
-        loads = ctx.enter_context(tc.tile_pool(name="loads", bufs=4))
-        quant = ctx.enter_context(tc.tile_pool(name="quant", bufs=4))
+        sb = ctx.enter_context(tc.tile_pool(name="sb", bufs=2))
         work = ctx.enter_context(tc.tile_pool(name="work", bufs=3))
-        psum_t = ctx.enter_context(tc.psum_pool(name="psum_t", bufs=2))
-        psum_z = ctx.enter_context(tc.psum_pool(name="psum_z", bufs=2))
-        psum_h = ctx.enter_context(tc.psum_pool(name="psum_h", bufs=4))
+        psum2 = ctx.enter_context(tc.psum_pool(name="psum2", bufs=2))
+        psum1 = ctx.enter_context(tc.psum_pool(name="psum1", bufs=1))
         ctx.enter_context(tc.manual_schedule())
 
-        h_tiles, x_tiles, a_tiles, aT_tiles = {}, {}, {}, {}
-        grouped_tiles, code_tiles, scale_tiles, xb_tiles = {}, {}, {}, {}
-        zp_tiles, diff0_tiles, hh1_tiles, gate_tiles, back1_tiles = {}, {}, {}, {}, {}
+        h_tiles, a_tiles, x_tiles, aT_tiles = {}, {}, {}, {}
+        grouped_tiles, code_tiles, scale_tiles, zT_tiles = {}, {}, {}, {}
+        zb_tiles, diff0_tiles, hh1_tiles, g_tiles, diff1_tiles = {}, {}, {}, {}, {}
 
-        def load_chunk(c):
-            h_tiles[c] = loads.tile([P, J, D], BF16, name="h_sb")
+        def load_state(c):
+            h_tiles[c] = sb.tile([P, J, D], BF16, name="h_sb", bufs=5)
             nc.sync.dma_start(out=h_tiles[c][:], in_=h_chunks[c])
-            a_tiles[c] = loads.tile([P, J, N * S], BF16, name="a_sb")
+            a_tiles[c] = sb.tile([P, J, N * S], BF16, name="a_sb")
             nc.sync.dma_start(out=a_tiles[c][:], in_=a_chunks[c])
-            x_tiles[c] = loads.tile([P, J, D], BF16, name="x_sb")
-            nc.sync.dma_start(out=x_tiles[c][:], in_=x_chunks[c])
 
-        load_chunk(0)
+        b_rows = const.tile([P, P], BF16)
+        nc.vector.memset(b_rows[:], 0.0)
+        nc.sync.dma_start(out=b_rows[0:BLOCKS, :], in_=b_g.rearrange("(r c) -> r c", c=P))
+        bg_rows = const.tile([P, 1], BF16)
+        nc.sync.dma_start(out=bg_rows[:], in_=bg.partition_broadcast(P))
+        h_tiles[0] = sb.tile([P, J, D], BF16, name="h_sb", bufs=5)
+        for j in range(J):
+            nc.sync.dma_start(out=h_tiles[0][:, j, :], in_=h_chunks[0][:, j, :])
+        a_tiles[0] = sb.tile([P, J, N * S], BF16, name="a_sb")
+        nc.sync.dma_start(out=a_tiles[0][:], in_=a_chunks[0])
 
         ident = const.tile([P, P], F32)
         make_identity(nc, ident[:])
+        ident_bf = const.tile([P, P], BF16)
+        make_identity(nc, ident_bf[:])
+        minus_ident = const.tile([P, P], BF16)
+        nc.vector.tensor_scalar_mul(out=minus_ident[:], in0=ident_bf[:], scalar1=-1.0)
 
         w_words = const.tile([P, G, 2 * D], U8, align_bytes=64)
         nc.sync.dma_start(
@@ -70,109 +85,130 @@ def tile_tpru_pb_t_kernel(tc, a, vr, h, x2g, w_g_words, w_g_scales, b_g, bg, out
                 out=w_planes[32 * quad : 32 * quad + 4].bitcast(I32),
                 in_=w_g_scales[:, 4 * quad : 4 * quad + 4, :].rearrange("g r n -> r g n").bitcast(I32),
             )
-        ident_bf = const.tile([P, P], BF16)
-        make_identity(nc, ident_bf[:])
-        minus_ident = const.tile([P, P], BF16)
-        nc.vector.tensor_scalar_mul(out=minus_ident[:], in0=ident_bf[:], scalar1=-1.0)
         vr_sb = const.tile([P, S, DS], BF16)
         nc.sync.dma_start(out=vr_sb[:], in_=vr)
 
-        b_rows = const.tile([P, D], BF16)
-        nc.sync.dma_start(out=b_rows[:], in_=b_g.partition_broadcast(P))
-        bg_rows = const.tile([P, 1], BF16)
-        nc.sync.dma_start(out=bg_rows[:], in_=bg.partition_broadcast(P))
-        bias = const.tile([P, D], F32)
-        nc.vector.tensor_tensor(out=bias[:], in0=b_rows[:], in1=bg_rows[:].to_broadcast([P, D]), op=ALU.add)
+        b_rows32 = const.tile([P, P], F32)
+        nc.vector.tensor_copy(out=b_rows32[:], in_=b_rows[:])
+        b_cols = psum2.tile([P, P], F32, tag="tp")
+        nc.tensor.transpose(b_cols[:], b_rows32[:], ident[:])
+        bias_cols = const.tile([P, BLOCKS], F32)
+        nc.vector.tensor_tensor(
+            out=bias_cols[:], in0=b_cols[:, 0:BLOCKS], in1=bg_rows[:].to_broadcast([P, BLOCKS]), op=ALU.add
+        )
 
-        def transpose(r):
-            c, j = divmod(r, J)
+        def transpose(t):
+            c, j = divmod(t, J)
             if j == 0:
                 if c + 1 < CHUNKS:
-                    load_chunk(c + 1)
-                at = psum_t.tile([P, J, P], F32, tag="tp")
+                    load_state(c + 1)
+                at = psum2.tile([P, J, P], F32, tag="tp")
                 for jj in range(J):
                     nc.tensor.transpose(at[:, jj, :], a_tiles[c][:, jj, :].bitcast(F32), ident[:])
-                aT_tiles[c] = loads.tile([P, S, J, P], BF16, name="aT")
+                aT_tiles[c] = sb.tile([P, S, J, P], BF16, name="aT", bufs=4)
                 nc.scalar.copy(out=aT_tiles[c][:], in_=at[:].bitcast(BF16).rearrange("n j (b s) -> n s j b", s=S))
             h_words = h_tiles[c][:, j, :].bitcast(F32)
-            ht = psum_t.tile([P, G, 2, P], F32, tag="tp")
+            ht = psum2.tile([P, G, 2, P], F32, tag="tp")
             for g in range(G):
                 for u in range(2):
                     nc.tensor.transpose(ht[:, g, u, :], h_words[:, 256 * g + u : 256 * (g + 1) : 2], ident[:])
-            grouped_tiles[r] = quant.tile([P, G, P, 2], F32, name="grouped", align_bytes=64)
-            nc.scalar.copy(out=grouped_tiles[r][:], in_=ht[:].rearrange("p g u b -> p g b u"))
+            grouped_tiles[t] = work.tile([P, G, P, 2], F32, name="grouped", align_bytes=64)
+            nc.scalar.copy(out=grouped_tiles[t][:], in_=ht[:].rearrange("p g u b -> p g b u"))
 
-        def quantise(r):
-            c, j = divmod(r, J)
-            code_tiles[r] = quant.tile([P, G, P], U32, name="codes", align_bytes=64)
-            scale_tiles[r] = quant.tile([P, G, P], U8, name="scales", align_bytes=64)
-            nc.vector.quantize_mx(
-                out=code_tiles[r][:].rearrange("p g b -> p (g b)").bitcast(FP8X4),
-                scales=scale_tiles[r][:].rearrange("p g b -> p (g b)"),
-                in_=grouped_tiles.pop(r)[:].rearrange("p g b u -> p (g b u)").bitcast(BF16),
-            )
-            xb_tiles[r] = quant.tile([P, D], F32, name="xb")
-            nc.gpsimd.tensor_tensor(out=xb_tiles[r][:], in0=x_tiles[c][:, j, :], in1=bias[:], op=ALU.add)
+        def quantise(t):
+            c, j = divmod(t, J)
+            if j == 0:
+                code_tiles[c] = sb.tile([P, G, ROWS], U32, name="codes", align_bytes=64)
+                scale_tiles[c] = sb.tile([P, G, ROWS], U8, name="scales", align_bytes=64)
+            grouped = grouped_tiles.pop(t)
+            rows = slice(P * j, P * (j + 1))
+            for g in range(G):
+                nc.vector.quantize_mx(
+                    out=code_tiles[c][:, g, rows].bitcast(FP8X4),
+                    scales=scale_tiles[c][:, g, rows],
+                    in_=grouped[:, g, :, :].rearrange("p b u -> p (b u)").bitcast(BF16),
+                )
 
-        def gate_matmuls(r):
-            codes, scales = code_tiles.pop(r), scale_tiles.pop(r)
-            for s in range(S):
-                zp = psum_z.tile([P, DS], F32, name="zp")
+        def gate_matmuls(m):
+            c, quarter = divmod(m, J)
+            if quarter == 0:
+                x_tiles[c] = sb.tile([P, J, D], BF16, name="x_sb", bufs=3)
+                nc.sync.dma_start(out=x_tiles[c][:], in_=x_chunks[c])
+                zT_tiles[c] = sb.tile([P, BLOCKS, ROWS], F32, name="zT")
+            for block in range(BLOCKS_A_TURN * quarter, BLOCKS_A_TURN * (quarter + 1)):
+                gt = psum2.tile([P, ROWS], F32, name="gt")
                 for g in range(G):
                     nc.tensor.matmul_mx(
-                        out=zp[:],
-                        lhsT=codes[:, g, :].bitcast(FP8X4),
-                        lhsT_scale=scales[:, g, :],
-                        rhs=w_words[:, g, 2 * DS * s : 2 * DS * (s + 1)].bitcast(FP4X4),
-                        rhs_scale=w_planes[:, g, DS * s : DS * (s + 1)],
+                        out=gt[:],
+                        lhsT=w_words[:, g, 2 * P * block : 2 * P * (block + 1)].bitcast(FP4X4),
+                        lhsT_scale=w_planes[:, g, P * block : P * (block + 1)],
+                        rhs=code_tiles[c][:, g, :].bitcast(FP8X4),
+                        rhs_scale=scale_tiles[c][:, g, :],
                         start=(g == 0),
                         stop=(g == G - 1),
                     )
-                zp_tiles[(r, s)] = zp
+                nc.scalar.activation(
+                    out=zT_tiles[c][:, block, :], in_=gt[:], func=ACT.Identity, bias=bias_cols[:, block : block + 1]
+                )
 
-        def role_matmuls(r):
+        def turn_back(r):
             c, j = divmod(r, J)
-            diff0 = psum_h.tile([P, DS], F32, tag="hh")
+            for s in range(S):
+                zb = psum2.tile([P, DS], F32, name="zb")
+                for q in range(DS // P):
+                    nc.tensor.transpose(
+                        zb[:, P * q : P * (q + 1)], zT_tiles[c][:, (DS // P) * s + q, P * j : P * (j + 1)], ident[:]
+                    )
+                zb_tiles[(r, s)] = zb
+
+        def roles_slice1(r):
+            c, j = divmod(r, J)
+            hh1_tiles[r] = psum1.tile([P, DS], F32, name="hh1")
+            nc.tensor.matmul(out=hh1_tiles[r][:], lhsT=aT_tiles[c][:, 1, j, :], rhs=vr_sb[:, 1, :], start=True, stop=True)
+
+        def roles_slice0(r):
+            c, j = divmod(r, J)
+            diff0 = psum1.tile([P, DS], F32, name="diff0")
             nc.tensor.matmul(out=diff0[:], lhsT=aT_tiles[c][:, 0, j, :], rhs=vr_sb[:, 0, :], start=True, stop=False)
             nc.tensor.matmul(out=diff0[:], lhsT=minus_ident[:], rhs=h_tiles[c][:, j, first], start=False, stop=True)
-            hh1 = psum_h.tile([P, DS], F32, tag="hh")
-            nc.tensor.matmul(out=hh1[:], lhsT=aT_tiles[c][:, 1, j, :], rhs=vr_sb[:, 1, :], start=True, stop=True)
-            diff0_tiles[r], hh1_tiles[r] = diff0, hh1
+            diff0_tiles[r] = diff0
 
         def gate(r):
             c, j = divmod(r, J)
-            xb = xb_tiles.pop(r)
             z = work.tile([P, D], F32, name="z")
-            g_sb = work.tile([P, D], F32, name="g_sb")
-            nc.vector.tensor_tensor(out=z[:, first], in0=zp_tiles.pop((r, 0))[:], in1=xb[:, first], op=ALU.add)
-            nc.scalar.activation(out=g_sb[:, first], in_=z[:, first], func=ACT.Sigmoid)
-            nc.vector.tensor_tensor(out=z[:, second], in0=zp_tiles.pop((r, 1))[:], in1=xb[:, second], op=ALU.add)
-            nc.scalar.activation(out=g_sb[:, second], in_=z[:, second], func=ACT.Sigmoid, scale=-1.0)
-            diff1 = work.tile([P, DS], F32, name="diff1")
-            nc.vector.tensor_tensor(out=diff1[:], in0=hh1_tiles[r][:], in1=h_tiles[c][:, j, second], op=ALU.subtract)
-            back1 = work.tile([P, DS], F32, name="back1")
-            nc.gpsimd.tensor_tensor(out=back1[:], in0=g_sb[:, second], in1=diff1[:], op=ALU.mult)
-            gate_tiles[r], back1_tiles[r] = g_sb, back1
+            nc.vector.tensor_tensor(out=z[:, first], in0=zb_tiles.pop((r, 0))[:], in1=x_tiles[c][:, j, first], op=ALU.add)
+            nc.vector.tensor_tensor(out=z[:, second], in0=zb_tiles.pop((r, 1))[:], in1=x_tiles[c][:, j, second], op=ALU.add)
+            g_tiles[r] = work.tile([P, D], F32, name="g_sb")
+            nc.scalar.activation(out=g_tiles[r][:], in_=z[:], func=ACT.Sigmoid)
+            diff1_tiles[r] = work.tile([P, DS], F32, name="diff1")
+            nc.vector.tensor_tensor(
+                out=diff1_tiles[r][:], in0=hh1_tiles.pop(r)[:], in1=h_tiles[c][:, j, second], op=ALU.subtract
+            )
 
         def blend(r):
             c, j = divmod(r, J)
+            g_sb = g_tiles.pop(r)
+            move = work.tile([P, D], F32, name="move")
+            nc.vector.tensor_tensor(out=move[:, first], in0=diff0_tiles.pop(r)[:], in1=g_sb[:, first], op=ALU.mult)
+            nc.vector.tensor_tensor(out=move[:, second], in0=diff1_tiles.pop(r)[:], in1=g_sb[:, second], op=ALU.mult)
             o_sb = work.tile([P, D], F32, name="o_sb")
-            move0 = work.tile([P, DS], F32, name="move0")
-            nc.vector.tensor_tensor(out=move0[:], in0=diff0_tiles.pop(r)[:], in1=gate_tiles.pop(r)[:, first], op=ALU.mult)
-            nc.vector.tensor_tensor(out=o_sb[:, first], in0=move0[:], in1=h_tiles[c][:, j, first], op=ALU.add)
-            nc.vector.tensor_tensor(out=o_sb[:, second], in0=hh1_tiles.pop(r)[:], in1=back1_tiles.pop(r)[:], op=ALU.subtract)
+            nc.vector.tensor_tensor(out=o_sb[:], in0=move[:], in1=h_tiles[c][:, j, :], op=ALU.add)
             nc.sync.dma_start(out=out_tiles[r], in_=o_sb[:])
 
-        for r in range(-3, ROW_TILES + 1):
+        for r in range(-TRANSPOSE_AHEAD, ROW_TILES + 1):
             if 0 <= r < ROW_TILES:
                 gate(r)
             if 0 <= r - 1:
                 blend(r - 1)
-            if 0 <= r + 2 < ROW_TILES:
-                quantise(r + 2)
             if 0 <= r + 1 < ROW_TILES:
-                gate_matmuls(r + 1)
-            if r + 3 < ROW_TILES:
-                transpose(r + 3)
+                turn_back(r + 1)
+            if r + TRANSPOSE_AHEAD < ROW_TILES:
+                transpose(r + TRANSPOSE_AHEAD)
             if 0 <= r + 1 < ROW_TILES:
-                role_matmuls(r + 1)
+                roles_slice1(r + 1)
+            if 0 <= r < ROW_TILES:
+                roles_slice0(r)
+            if 0 <= r + MATMUL_AHEAD < ROW_TILES:
+                gate_matmuls(r + MATMUL_AHEAD)
+            if 0 <= r + QUANTISE_AHEAD < ROW_TILES:
+                quantise(r + QUANTISE_AHEAD)

@@ -44,11 +44,12 @@ def tile_tpru_pb_t_kernel(tc, a, vr, h, x2g, w_g_words, w_g_scales, b_g, bg, out
         work = ctx.enter_context(tc.tile_pool(name="work", bufs=3))
         psum2 = ctx.enter_context(tc.psum_pool(name="psum2", bufs=2))
         psum1 = ctx.enter_context(tc.psum_pool(name="psum1", bufs=1))
+        psum3 = ctx.enter_context(tc.psum_pool(name="psum3", bufs=3))
         ctx.enter_context(tc.manual_schedule())
 
         h_tiles, a_tiles, x_tiles, aT_tiles = {}, {}, {}, {}
         grouped_tiles, code_tiles, scale_tiles, zT_tiles = {}, {}, {}, {}
-        zb_tiles, diff0_tiles, hh1_tiles, g_tiles, diff1_tiles = {}, {}, {}, {}, {}
+        zb_tiles, diff0_tiles, hh1_tiles, g_tiles, back1_tiles = {}, {}, {}, {}, {}
 
         def load_state(c):
             h_tiles[c] = sb.tile([P, J, D], BF16, name="h_sb", bufs=5)
@@ -61,11 +62,11 @@ def tile_tpru_pb_t_kernel(tc, a, vr, h, x2g, w_g_words, w_g_scales, b_g, bg, out
         nc.sync.dma_start(out=b_rows[0:BLOCKS, :], in_=b_g.rearrange("(r c) -> r c", c=P))
         bg_rows = const.tile([P, 1], BF16)
         nc.sync.dma_start(out=bg_rows[:], in_=bg.partition_broadcast(P))
+        a_tiles[0] = sb.tile([P, J, N * S], BF16, name="a_sb")
+        nc.sync.dma_start(out=a_tiles[0][:], in_=a_chunks[0])
         h_tiles[0] = sb.tile([P, J, D], BF16, name="h_sb", bufs=5)
         for j in range(J):
             nc.sync.dma_start(out=h_tiles[0][:, j, :], in_=h_chunks[0][:, j, :])
-        a_tiles[0] = sb.tile([P, J, N * S], BF16, name="a_sb")
-        nc.sync.dma_start(out=a_tiles[0][:], in_=a_chunks[0])
 
         ident = const.tile([P, P], F32)
         make_identity(nc, ident[:])
@@ -90,7 +91,7 @@ def tile_tpru_pb_t_kernel(tc, a, vr, h, x2g, w_g_words, w_g_scales, b_g, bg, out
 
         b_rows32 = const.tile([P, P], F32)
         nc.vector.tensor_copy(out=b_rows32[:], in_=b_rows[:])
-        b_cols = psum2.tile([P, P], F32, tag="tp")
+        b_cols = psum2.tile([P, P], F32, tag="gt")
         nc.tensor.transpose(b_cols[:], b_rows32[:], ident[:])
         bias_cols = const.tile([P, BLOCKS], F32)
         nc.vector.tensor_tensor(
@@ -102,13 +103,13 @@ def tile_tpru_pb_t_kernel(tc, a, vr, h, x2g, w_g_words, w_g_scales, b_g, bg, out
             if j == 0:
                 if c + 1 < CHUNKS:
                     load_state(c + 1)
-                at = psum2.tile([P, J, P], F32, tag="tp")
+                at = psum2.tile([P, J, P], F32, tag="gt")
                 for jj in range(J):
                     nc.tensor.transpose(at[:, jj, :], a_tiles[c][:, jj, :].bitcast(F32), ident[:])
                 aT_tiles[c] = sb.tile([P, S, J, P], BF16, name="aT", bufs=4)
                 nc.scalar.copy(out=aT_tiles[c][:], in_=at[:].bitcast(BF16).rearrange("n j (b s) -> n s j b", s=S))
             h_words = h_tiles[c][:, j, :].bitcast(F32)
-            ht = psum2.tile([P, G, 2, P], F32, tag="tp")
+            ht = psum3.tile([P, G, 2, P], F32, tag="turn")
             for g in range(G):
                 for u in range(2):
                     nc.tensor.transpose(ht[:, g, u, :], h_words[:, 256 * g + u : 256 * (g + 1) : 2], ident[:])
@@ -136,7 +137,7 @@ def tile_tpru_pb_t_kernel(tc, a, vr, h, x2g, w_g_words, w_g_scales, b_g, bg, out
                 nc.sync.dma_start(out=x_tiles[c][:], in_=x_chunks[c])
                 zT_tiles[c] = sb.tile([P, BLOCKS, ROWS], F32, name="zT")
             for block in range(BLOCKS_A_TURN * quarter, BLOCKS_A_TURN * (quarter + 1)):
-                gt = psum2.tile([P, ROWS], F32, name="gt")
+                gt = psum2.tile([P, ROWS], F32, tag="gt")
                 for g in range(G):
                     nc.tensor.matmul_mx(
                         out=gt[:],
@@ -154,7 +155,7 @@ def tile_tpru_pb_t_kernel(tc, a, vr, h, x2g, w_g_words, w_g_scales, b_g, bg, out
         def turn_back(r):
             c, j = divmod(r, J)
             for s in range(S):
-                zb = psum2.tile([P, DS], F32, name="zb")
+                zb = psum3.tile([P, DS], F32, tag="turn")
                 for q in range(DS // P):
                     nc.tensor.transpose(
                         zb[:, P * q : P * (q + 1)], zT_tiles[c][:, (DS // P) * s + q, P * j : P * (j + 1)], ident[:]
@@ -163,7 +164,7 @@ def tile_tpru_pb_t_kernel(tc, a, vr, h, x2g, w_g_words, w_g_scales, b_g, bg, out
 
         def roles_slice1(r):
             c, j = divmod(r, J)
-            hh1_tiles[r] = psum1.tile([P, DS], F32, name="hh1")
+            hh1_tiles[r] = psum2.tile([P, DS], F32, name="hh1")
             nc.tensor.matmul(out=hh1_tiles[r][:], lhsT=aT_tiles[c][:, 1, j, :], rhs=vr_sb[:, 1, :], start=True, stop=True)
 
         def roles_slice0(r):
@@ -176,23 +177,24 @@ def tile_tpru_pb_t_kernel(tc, a, vr, h, x2g, w_g_words, w_g_scales, b_g, bg, out
         def gate(r):
             c, j = divmod(r, J)
             z = work.tile([P, D], F32, name="z")
+            g_sb = work.tile([P, D], F32, name="g_sb")
             nc.vector.tensor_tensor(out=z[:, first], in0=zb_tiles.pop((r, 0))[:], in1=x_tiles[c][:, j, first], op=ALU.add)
+            nc.scalar.activation(out=g_sb[:, first], in_=z[:, first], func=ACT.Sigmoid)
             nc.vector.tensor_tensor(out=z[:, second], in0=zb_tiles.pop((r, 1))[:], in1=x_tiles[c][:, j, second], op=ALU.add)
-            g_tiles[r] = work.tile([P, D], F32, name="g_sb")
-            nc.scalar.activation(out=g_tiles[r][:], in_=z[:], func=ACT.Sigmoid)
-            diff1_tiles[r] = work.tile([P, DS], F32, name="diff1")
-            nc.vector.tensor_tensor(
-                out=diff1_tiles[r][:], in0=hh1_tiles.pop(r)[:], in1=h_tiles[c][:, j, second], op=ALU.subtract
-            )
+            nc.scalar.activation(out=g_sb[:, second], in_=z[:, second], func=ACT.Sigmoid, scale=-1.0)
+            diff1 = work.tile([P, DS], F32, name="diff1")
+            nc.vector.tensor_tensor(out=diff1[:], in0=hh1_tiles[r][:], in1=h_tiles[c][:, j, second], op=ALU.subtract)
+            back1_tiles[r] = work.tile([P, DS], F32, name="back1")
+            nc.gpsimd.tensor_tensor(out=back1_tiles[r][:], in0=g_sb[:, second], in1=diff1[:], op=ALU.mult)
+            g_tiles[r] = g_sb
 
         def blend(r):
             c, j = divmod(r, J)
-            g_sb = g_tiles.pop(r)
-            move = work.tile([P, D], F32, name="move")
-            nc.vector.tensor_tensor(out=move[:, first], in0=diff0_tiles.pop(r)[:], in1=g_sb[:, first], op=ALU.mult)
-            nc.vector.tensor_tensor(out=move[:, second], in0=diff1_tiles.pop(r)[:], in1=g_sb[:, second], op=ALU.mult)
             o_sb = work.tile([P, D], F32, name="o_sb")
-            nc.vector.tensor_tensor(out=o_sb[:], in0=move[:], in1=h_tiles[c][:, j, :], op=ALU.add)
+            move0 = work.tile([P, DS], F32, name="move0")
+            nc.vector.tensor_tensor(out=move0[:], in0=diff0_tiles.pop(r)[:], in1=g_tiles.pop(r)[:, first], op=ALU.mult)
+            nc.gpsimd.tensor_tensor(out=o_sb[:, first], in0=move0[:], in1=h_tiles[c][:, j, first], op=ALU.add)
+            nc.vector.tensor_tensor(out=o_sb[:, second], in0=hh1_tiles.pop(r)[:], in1=back1_tiles.pop(r)[:], op=ALU.subtract)
             nc.sync.dma_start(out=out_tiles[r], in_=o_sb[:])
 
         for r in range(-TRANSPOSE_AHEAD, ROW_TILES + 1):
@@ -202,13 +204,13 @@ def tile_tpru_pb_t_kernel(tc, a, vr, h, x2g, w_g_words, w_g_scales, b_g, bg, out
                 blend(r - 1)
             if 0 <= r + 1 < ROW_TILES:
                 turn_back(r + 1)
-            if r + TRANSPOSE_AHEAD < ROW_TILES:
-                transpose(r + TRANSPOSE_AHEAD)
-            if 0 <= r + 1 < ROW_TILES:
-                roles_slice1(r + 1)
             if 0 <= r < ROW_TILES:
                 roles_slice0(r)
             if 0 <= r + MATMUL_AHEAD < ROW_TILES:
                 gate_matmuls(r + MATMUL_AHEAD)
+            if r + TRANSPOSE_AHEAD < ROW_TILES:
+                transpose(r + TRANSPOSE_AHEAD)
+            if 0 <= r + 1 < ROW_TILES:
+                roles_slice1(r + 1)
             if 0 <= r + QUANTISE_AHEAD < ROW_TILES:
                 quantise(r + QUANTISE_AHEAD)

@@ -52,21 +52,18 @@ def tile_tpru_pb_t_kernel(tc, a, vr, h, x2g, w_g_words, w_g_scales, b_g, bg, out
         zb_tiles, diff0_tiles, hh1_tiles, g_tiles, back1_tiles = {}, {}, {}, {}, {}
 
         def load_state(c):
-            h_tiles[c] = sb.tile([P, J, D], BF16, name="h_sb", bufs=5)
-            nc.sync.dma_start(out=h_tiles[c][:], in_=h_chunks[c])
             a_tiles[c] = sb.tile([P, J, N * S], BF16, name="a_sb")
             nc.sync.dma_start(out=a_tiles[c][:], in_=a_chunks[c])
+            h_tiles[c] = sb.tile([P, J, D], BF16, name="h_sb", bufs=5)
+            for j in range(J):
+                nc.sync.dma_start(out=h_tiles[c][:, j, :], in_=h_chunks[c][:, j, :])
 
         b_rows = const.tile([P, P], BF16)
         nc.vector.memset(b_rows[:], 0.0)
         nc.sync.dma_start(out=b_rows[0:BLOCKS, :], in_=b_g.rearrange("(r c) -> r c", c=P))
         bg_rows = const.tile([P, 1], BF16)
         nc.sync.dma_start(out=bg_rows[:], in_=bg.partition_broadcast(P))
-        a_tiles[0] = sb.tile([P, J, N * S], BF16, name="a_sb")
-        nc.sync.dma_start(out=a_tiles[0][:], in_=a_chunks[0])
-        h_tiles[0] = sb.tile([P, J, D], BF16, name="h_sb", bufs=5)
-        for j in range(J):
-            nc.sync.dma_start(out=h_tiles[0][:, j, :], in_=h_chunks[0][:, j, :])
+        load_state(0)
 
         ident = const.tile([P, P], F32)
         make_identity(nc, ident[:])
@@ -204,12 +201,12 @@ def tile_tpru_pb_t_kernel(tc, a, vr, h, x2g, w_g_words, w_g_scales, b_g, bg, out
                 blend(r - 1)
             if 0 <= r + 1 < ROW_TILES:
                 turn_back(r + 1)
-            if 0 <= r < ROW_TILES:
-                roles_slice0(r)
-            if 0 <= r + MATMUL_AHEAD < ROW_TILES:
-                gate_matmuls(r + MATMUL_AHEAD)
             if r + TRANSPOSE_AHEAD < ROW_TILES:
                 transpose(r + TRANSPOSE_AHEAD)
+            if 0 <= r + MATMUL_AHEAD < ROW_TILES:
+                gate_matmuls(r + MATMUL_AHEAD)
+            if 0 <= r < ROW_TILES:
+                roles_slice0(r)
             if 0 <= r + 1 < ROW_TILES:
                 roles_slice1(r + 1)
             if 0 <= r + QUANTISE_AHEAD < ROW_TILES:

@@ -171,7 +171,7 @@ def tile_tpru_pb_t_kernel(tc, a, vr, h, x2g, w_g_words, w_g_scales, b_g, bg, out
             nc.tensor.matmul(out=diff0[:], lhsT=minus_ident[:], rhs=h_tiles[c][:, j, first], start=False, stop=True)
             diff0_tiles[r] = diff0
 
-        def gate(r):
+        def gate_sums(r):
             c, j = divmod(r, J)
             z = work.tile([P, D], F32, name="z")
             g_sb = work.tile([P, D], F32, name="g_sb")
@@ -179,11 +179,15 @@ def tile_tpru_pb_t_kernel(tc, a, vr, h, x2g, w_g_words, w_g_scales, b_g, bg, out
             nc.scalar.activation(out=g_sb[:, first], in_=z[:, first], func=ACT.Sigmoid)
             nc.vector.tensor_tensor(out=z[:, second], in0=zb_tiles.pop((r, 1))[:], in1=x_tiles[c][:, j, second], op=ALU.add)
             nc.scalar.activation(out=g_sb[:, second], in_=z[:, second], func=ACT.Sigmoid, scale=-1.0)
+            g_tiles[r] = g_sb
+
+        def gate_rest(r):
+            c, j = divmod(r, J)
+            g_sb = g_tiles[r]
             diff1 = work.tile([P, DS], F32, name="diff1")
             nc.vector.tensor_tensor(out=diff1[:], in0=hh1_tiles[r][:], in1=h_tiles[c][:, j, second], op=ALU.subtract)
             back1_tiles[r] = work.tile([P, DS], F32, name="back1")
             nc.gpsimd.tensor_tensor(out=back1_tiles[r][:], in0=g_sb[:, second], in1=diff1[:], op=ALU.mult)
-            g_tiles[r] = g_sb
 
         def blend(r):
             c, j = divmod(r, J)
@@ -196,7 +200,11 @@ def tile_tpru_pb_t_kernel(tc, a, vr, h, x2g, w_g_words, w_g_scales, b_g, bg, out
 
         for r in range(-TRANSPOSE_AHEAD, ROW_TILES + 1):
             if 0 <= r < ROW_TILES:
-                gate(r)
+                gate_sums(r)
+            if 0 <= r + QUANTISE_AHEAD < ROW_TILES:
+                quantise(r + QUANTISE_AHEAD)
+            if 0 <= r < ROW_TILES:
+                gate_rest(r)
             if 0 <= r - 1:
                 blend(r - 1)
             if 0 <= r + 1 < ROW_TILES:
@@ -209,5 +217,3 @@ def tile_tpru_pb_t_kernel(tc, a, vr, h, x2g, w_g_words, w_g_scales, b_g, bg, out
                 roles_slice0(r)
             if 0 <= r + 1 < ROW_TILES:
                 roles_slice1(r + 1)
-            if 0 <= r + QUANTISE_AHEAD < ROW_TILES:
-                quantise(r + QUANTISE_AHEAD)

@@ -110,22 +110,20 @@ def tile_tpru_pb_t_kernel(tc, a, vr, h, x2g, w_g_words, w_g_scales, b_g, bg, out
             for g in range(G):
                 for u in range(2):
                     nc.tensor.transpose(ht[:, g, u, :], h_words[:, 256 * g + u : 256 * (g + 1) : 2], ident[:])
-            grouped_tiles[t] = work.tile([P, G, P, 2], F32, name="grouped", align_bytes=64)
-            nc.scalar.copy(out=grouped_tiles[t][:], in_=ht[:].rearrange("p g u b -> p g b u"))
-
-        def quantise(t):
-            c, j = divmod(t, J)
             if j == 0:
-                code_tiles[c] = sb.tile([P, G, ROWS], U32, name="codes", align_bytes=64)
-                scale_tiles[c] = sb.tile([P, G, ROWS], U8, name="scales", align_bytes=64)
-            grouped = grouped_tiles.pop(t)
-            rows = slice(P * j, P * (j + 1))
-            for g in range(G):
-                nc.vector.quantize_mx(
-                    out=code_tiles[c][:, g, rows].bitcast(FP8X4),
-                    scales=scale_tiles[c][:, g, rows],
-                    in_=grouped[:, g, :, :].rearrange("p b u -> p (b u)").bitcast(BF16),
-                )
+                grouped_tiles[c] = sb.tile([P, G, ROWS, 2], F32, name="grouped", align_bytes=64)
+            nc.scalar.copy(
+                out=grouped_tiles[c][:, :, P * j : P * (j + 1), :], in_=ht[:].rearrange("p g u b -> p g b u")
+            )
+
+        def quantise(c):
+            code_tiles[c] = sb.tile([P, G, ROWS], U32, name="codes", align_bytes=64)
+            scale_tiles[c] = sb.tile([P, G, ROWS], U8, name="scales", align_bytes=64)
+            nc.vector.quantize_mx(
+                out=code_tiles[c][:].rearrange("p g b -> p (g b)").bitcast(FP8X4),
+                scales=scale_tiles[c][:].rearrange("p g b -> p (g b)"),
+                in_=grouped_tiles.pop(c)[:].rearrange("p g b u -> p (g b u)").bitcast(BF16),
+            )
 
         def gate_matmuls(m):
             c, quarter = divmod(m, J)
@@ -201,8 +199,8 @@ def tile_tpru_pb_t_kernel(tc, a, vr, h, x2g, w_g_words, w_g_scales, b_g, bg, out
         for r in range(-TRANSPOSE_AHEAD, ROW_TILES + 1):
             if 0 <= r < ROW_TILES:
                 gate_sums(r)
-            if 0 <= r + QUANTISE_AHEAD < ROW_TILES:
-                quantise(r + QUANTISE_AHEAD)
+            if 0 <= r + QUANTISE_AHEAD < ROW_TILES and (r + QUANTISE_AHEAD) % J == J - 1:
+                quantise((r + QUANTISE_AHEAD) // J)
             if 0 <= r < ROW_TILES:
                 gate_rest(r)
             if 0 <= r - 1:

@@ -205,13 +205,13 @@ def tile_tpru_pb_t_kernel(tc, a, vr, h, x2g, w_g_words, w_g_scales, b_g, bg, out
                 gate_rest(r)
             if 0 <= r - 1:
                 blend(r - 1)
-            if 0 <= r + 1 < ROW_TILES:
-                turn_back(r + 1)
             if r + TRANSPOSE_AHEAD < ROW_TILES:
                 transpose(r + TRANSPOSE_AHEAD)
+            if 0 <= r + 1 < ROW_TILES:
+                turn_back(r + 1)
             if 0 <= r + MATMUL_AHEAD < ROW_TILES:
                 gate_matmuls(r + MATMUL_AHEAD)
-            if 0 <= r < ROW_TILES:
-                roles_slice0(r)
             if 0 <= r + 1 < ROW_TILES:
                 roles_slice1(r + 1)
+            if 0 <= r < ROW_TILES:
+                roles_slice0(r)

@@ -32,10 +32,10 @@ FLOPS = 2 * B * D * D + 2 * B * N * D
 
 def tile_tpru_pb_t_kernel(tc, a, vr, h, x2g, w_g_words, w_g_scales, b_g, bg, out):
     nc = tc.nc
-    h_chunks = h.rearrange("(c j p) k -> c p j k", p=P, j=J)
-    x_chunks = x2g.rearrange("(c j p) k -> c p j k", p=P, j=J)
-    a_chunks = a.rearrange("(c j p) n s -> c p j (n s)", p=P, j=J)
-    out_tiles = out.rearrange("(r p) k -> r p k", p=P)
+    h_chunks = h.rearrange("(c p j) k -> c p j k", p=P, j=J)
+    x_chunks = x2g.rearrange("(c p j) k -> c p j k", p=P, j=J)
+    a_chunks = a.rearrange("(c p j) n s -> c p j (n s)", p=P, j=J)
+    out_chunks = out.rearrange("(c p j) k -> c j p k", p=P, j=J)
     first, second = slice(0, DS), slice(DS, D)
 
     with ExitStack() as ctx:
@@ -55,27 +55,22 @@ def tile_tpru_pb_t_kernel(tc, a, vr, h, x2g, w_g_words, w_g_scales, b_g, bg, out
             a_tiles[c] = sb.tile([P, J, N * S], BF16, name="a_sb")
             nc.sync.dma_start(out=a_tiles[c][:], in_=a_chunks[c])
             h_tiles[c] = sb.tile([P, J, D], BF16, name="h_sb", bufs=5)
-            for j in range(J):
-                nc.sync.dma_start(out=h_tiles[c][:, j, :], in_=h_chunks[c][:, j, :])
+            if c == 0:
+                for j in range(J):
+                    nc.sync.dma_start(out=h_tiles[c][:, j, :], in_=h_chunks[c][:, j, :])
+            else:
+                nc.sync.dma_start(out=h_tiles[c][:], in_=h_chunks[c])
 
+        load_state(0)
+        w_words = const.tile([P, G, 2 * D], U8, align_bytes=64)
+        nc.sync.dma_start(
+            out=w_words[:].bitcast(I32), in_=w_g_words.rearrange("g p c -> p g c").bitcast(I32)
+        )
         b_rows = const.tile([P, P], BF16)
         nc.vector.memset(b_rows[:], 0.0)
         nc.sync.dma_start(out=b_rows[0:BLOCKS, :], in_=b_g.rearrange("(r c) -> r c", c=P))
         bg_rows = const.tile([P, 1], BF16)
         nc.sync.dma_start(out=bg_rows[:], in_=bg.partition_broadcast(P))
-        load_state(0)
-
-        ident = const.tile([P, P], F32)
-        make_identity(nc, ident[:])
-        ident_bf = const.tile([P, P], BF16)
-        make_identity(nc, ident_bf[:])
-        minus_ident = const.tile([P, P], BF16)
-        nc.vector.tensor_scalar_mul(out=minus_ident[:], in0=ident_bf[:], scalar1=-1.0)
-
-        w_words = const.tile([P, G, 2 * D], U8, align_bytes=64)
-        nc.sync.dma_start(
-            out=w_words[:].bitcast(I32), in_=w_g_words.rearrange("g p c -> p g c").bitcast(I32)
-        )
         w_planes = const.tile([P, G, D], U8, align_bytes=64)
         nc.vector.memset(w_planes[:].bitcast(I32), 0)
         for quad in range(4):
@@ -86,14 +81,27 @@ def tile_tpru_pb_t_kernel(tc, a, vr, h, x2g, w_g_words, w_g_scales, b_g, bg, out
         vr_sb = const.tile([P, S, DS], BF16)
         nc.sync.dma_start(out=vr_sb[:], in_=vr)
 
+        ident = const.tile([P, P], F32)
+        make_identity(nc, ident[:])
+        ident_bf = const.tile([P, P], BF16)
+        make_identity(nc, ident_bf[:])
+        minus_ident = const.tile([P, P], BF16)
+        nc.vector.tensor_scalar_mul(out=minus_ident[:], in0=ident_bf[:], scalar1=-1.0)
+        zero_col = const.tile([P, 1], F32)
+        nc.vector.memset(zero_col[:], 0.0)
+        half_col = const.tile([P, 1], F32)
+        nc.scalar.activation(out=half_col[:], in_=zero_col[:], func=ACT.Sigmoid)
+
         b_rows32 = const.tile([P, P], F32)
         nc.vector.tensor_copy(out=b_rows32[:], in_=b_rows[:])
-        b_cols = psum2.tile([P, P], F32, tag="gt")
-        nc.tensor.transpose(b_cols[:], b_rows32[:], ident[:])
         bias_cols = const.tile([P, BLOCKS], F32)
-        nc.vector.tensor_tensor(
-            out=bias_cols[:], in0=b_cols[:, 0:BLOCKS], in1=bg_rows[:].to_broadcast([P, BLOCKS]), op=ALU.add
-        )
+
+        def bias_columns():
+            b_cols = psum2.tile([P, P], F32, tag="gt")
+            nc.tensor.transpose(b_cols[:], b_rows32[:], ident[:])
+            nc.vector.tensor_tensor(
+                out=bias_cols[:], in0=b_cols[:, 0:BLOCKS], in1=bg_rows[:].to_broadcast([P, BLOCKS]), op=ALU.add
+            )
 
         def transpose(t):
             c, j = divmod(t, J)
@@ -192,9 +200,15 @@ def tile_tpru_pb_t_kernel(tc, a, vr, h, x2g, w_g_words, w_g_scales, b_g, bg, out
             o_sb = work.tile([P, D], F32, name="o_sb")
             move0 = work.tile([P, DS], F32, name="move0")
             nc.vector.tensor_tensor(out=move0[:], in0=diff0_tiles.pop(r)[:], in1=g_tiles.pop(r)[:, first], op=ALU.mult)
-            nc.gpsimd.tensor_tensor(out=o_sb[:, first], in0=move0[:], in1=h_tiles[c][:, j, first], op=ALU.add)
+            if r < ROW_TILES - 1:
+                nc.gpsimd.tensor_tensor(out=o_sb[:, first], in0=move0[:], in1=h_tiles[c][:, j, first], op=ALU.add)
             nc.vector.tensor_tensor(out=o_sb[:, second], in0=hh1_tiles.pop(r)[:], in1=back1_tiles.pop(r)[:], op=ALU.subtract)
-            nc.sync.dma_start(out=out_tiles[r], in_=o_sb[:])
+            if r < ROW_TILES - 1:
+                nc.sync.dma_start(out=out_chunks[c][j], in_=o_sb[:])
+            else:
+                nc.sync.dma_start(out=out_chunks[c][j][:, second], in_=o_sb[:, second])
+                nc.vector.tensor_tensor(out=o_sb[:, first], in0=move0[:], in1=h_tiles[c][:, j, first], op=ALU.add)
+                nc.sync.dma_start(out=out_chunks[c][j][:, first], in_=o_sb[:, first])
 
         for r in range(-TRANSPOSE_AHEAD, ROW_TILES + 1):
             if 0 <= r < ROW_TILES:
@@ -207,6 +221,8 @@ def tile_tpru_pb_t_kernel(tc, a, vr, h, x2g, w_g_words, w_g_scales, b_g, bg, out
                 blend(r - 1)
             if r + TRANSPOSE_AHEAD < ROW_TILES:
                 transpose(r + TRANSPOSE_AHEAD)
+            if r + MATMUL_AHEAD == -1:
+                bias_columns()
             if 0 <= r + 1 < ROW_TILES:
                 turn_back(r + 1)
             if 0 <= r + MATMUL_AHEAD < ROW_TILES:

@@ -26,6 +26,7 @@ BLOCKS_A_TURN = BLOCKS // J
 TRANSPOSE_AHEAD = 10
 QUANTISE_AHEAD = 9
 MATMUL_AHEAD = 5
+TILEWISE_CHUNKS = -(-TRANSPOSE_AHEAD // J)
 
 FLOPS = 2 * B * D * D + 2 * B * N * D
 
@@ -55,7 +56,7 @@ def tile_tpru_pb_t_kernel(tc, a, vr, h, x2g, w_g_words, w_g_scales, b_g, bg, out
             a_tiles[c] = sb.tile([P, J, N * S], BF16, name="a_sb")
             nc.sync.dma_start(out=a_tiles[c][:], in_=a_chunks[c])
             h_tiles[c] = sb.tile([P, J, D], BF16, name="h_sb", bufs=5)
-            if c == 0:
+            if c < TILEWISE_CHUNKS:
                 for j in range(J):
                     nc.sync.dma_start(out=h_tiles[c][:, j, :], in_=h_chunks[c][:, j, :])
             else:

@@ -26,7 +26,9 @@ BLOCKS_A_TURN = BLOCKS // J
 TRANSPOSE_AHEAD = 10
 QUANTISE_AHEAD = 9
 MATMUL_AHEAD = 5
-TILEWISE_CHUNKS = -(-TRANSPOSE_AHEAD // J)
+FIRST = J
+TRANSPOSE_AHEAD_FIRST = 3
+QUANTISE_AHEAD_FIRST = 2
 
 FLOPS = 2 * B * D * D + 2 * B * N * D
 
@@ -50,52 +52,81 @@ def tile_tpru_pb_t_kernel(tc, a, vr, h, x2g, w_g_words, w_g_scales, b_g, bg, out
 
         h_tiles, a_tiles, x_tiles, aT_tiles = {}, {}, {}, {}
         grouped_tiles, code_tiles, scale_tiles, zT_tiles = {}, {}, {}, {}
-        zb_tiles, diff0_tiles, hh1_tiles, g_tiles, back1_tiles = {}, {}, {}, {}, {}
+        zb_tiles, diff0_tiles, hh1_tiles, g_tiles, back1_tiles, xb_tiles = {}, {}, {}, {}, {}, {}
 
-        def load_state(c):
-            a_tiles[c] = sb.tile([P, J, N * S], BF16, name="a_sb")
-            nc.sync.dma_start(out=a_tiles[c][:], in_=a_chunks[c])
+        def state_tiles(c):
+            a_tiles[c] = sb.tile([P, J, N * S], BF16, name="a_sb", bufs=3)
             h_tiles[c] = sb.tile([P, J, D], BF16, name="h_sb", bufs=5)
-            if c < TILEWISE_CHUNKS:
-                for j in range(J):
-                    nc.sync.dma_start(out=h_tiles[c][:, j, :], in_=h_chunks[c][:, j, :])
-            else:
-                nc.sync.dma_start(out=h_tiles[c][:], in_=h_chunks[c])
 
-        load_state(0)
-        w_words = const.tile([P, G, 2 * D], U8, align_bytes=64)
-        nc.sync.dma_start(
-            out=w_words[:].bitcast(I32), in_=w_g_words.rearrange("g p c -> p g c").bitcast(I32)
-        )
+        def load_a(c):
+            nc.sync.dma_start(out=a_tiles[c][:], in_=a_chunks[c])
+
+        def load_h(t):
+            c, j = divmod(t, J)
+            nc.sync.dma_start(out=h_tiles[c][:, j, :], in_=h_chunks[c][:, j, :])
+
+        def load_x_first(j):
+            if j == 0:
+                x_tiles[0] = sb.tile([P, J, D], BF16, name="x_sb", bufs=3)
+            nc.sync.dma_start(out=x_tiles[0][:, j, :], in_=x_chunks[0][:, j, :])
+
         b_rows = const.tile([P, P], BF16)
         nc.vector.memset(b_rows[:], 0.0)
-        nc.sync.dma_start(out=b_rows[0:BLOCKS, :], in_=b_g.rearrange("(r c) -> r c", c=P))
-        bg_rows = const.tile([P, 1], BF16)
-        nc.sync.dma_start(out=bg_rows[:], in_=bg.partition_broadcast(P))
         w_planes = const.tile([P, G, D], U8, align_bytes=64)
         nc.vector.memset(w_planes[:].bitcast(I32), 0)
-        for quad in range(4):
-            nc.sync.dma_start(
-                out=w_planes[32 * quad : 32 * quad + 4].bitcast(I32),
-                in_=w_g_scales[:, 4 * quad : 4 * quad + 4, :].rearrange("g r n -> r g n").bitcast(I32),
-            )
-        vr_sb = const.tile([P, S, DS], BF16)
-        nc.sync.dma_start(out=vr_sb[:], in_=vr)
-
         ident = const.tile([P, P], F32)
         make_identity(nc, ident[:])
         ident_bf = const.tile([P, P], BF16)
         make_identity(nc, ident_bf[:])
         minus_ident = const.tile([P, P], BF16)
         nc.vector.tensor_scalar_mul(out=minus_ident[:], in0=ident_bf[:], scalar1=-1.0)
+
         zero_col = const.tile([P, 1], F32)
         nc.vector.memset(zero_col[:], 0.0)
         half_col = const.tile([P, 1], F32)
         nc.scalar.activation(out=half_col[:], in_=zero_col[:], func=ACT.Sigmoid)
 
+        for c in range(3):
+            state_tiles(c)
+        load_a(1)
+        load_h(FIRST)
+        load_h(FIRST + 1)
+        nc.sync.dma_start(out=b_rows[0:BLOCKS, :], in_=b_g.rearrange("(r c) -> r c", c=P))
+        bg_rows = const.tile([P, 1], BF16)
+        nc.sync.dma_start(out=bg_rows[:], in_=bg.partition_broadcast(P))
+        load_h(FIRST + 2)
+        load_h(FIRST + 3)
+        load_a(0)
+        load_h(0)
+        w_words = const.tile([P, G, 2 * D], U8, align_bytes=64)
+        nc.sync.dma_start(
+            out=w_words[:].bitcast(I32), in_=w_g_words.rearrange("g p c -> p g c").bitcast(I32)
+        )
+        for quad in range(4):
+            nc.sync.dma_start(
+                out=w_planes[32 * quad : 32 * quad + 4].bitcast(I32),
+                in_=w_g_scales[:, 4 * quad : 4 * quad + 4, :].rearrange("g r n -> r g n").bitcast(I32),
+            )
+        load_x_first(0)
+        load_a(2)
+        load_h(2 * FIRST)
+        load_h(1)
+        vr_sb = const.tile([P, S, DS], BF16)
+        nc.sync.dma_start(out=vr_sb[:], in_=vr)
+        load_h(2 * FIRST + 1)
+        load_h(2)
+        load_x_first(1)
+        load_h(2 * FIRST + 2)
+        load_h(3)
+        load_x_first(2)
+        load_h(2 * FIRST + 3)
+        load_x_first(3)
+
         b_rows32 = const.tile([P, P], F32)
         nc.vector.tensor_copy(out=b_rows32[:], in_=b_rows[:])
         bias_cols = const.tile([P, BLOCKS], F32)
+        bias_rows = const.tile([P, D], F32)
+        spread = const.tile([P, BLOCKS, P], F32)
 
         def bias_columns():
             b_cols = psum2.tile([P, P], F32, tag="gt")
@@ -103,12 +134,22 @@ def tile_tpru_pb_t_kernel(tc, a, vr, h, x2g, w_g_words, w_g_scales, b_g, bg, out
             nc.vector.tensor_tensor(
                 out=bias_cols[:], in0=b_cols[:, 0:BLOCKS], in1=bg_rows[:].to_broadcast([P, BLOCKS]), op=ALU.add
             )
+            nc.vector.tensor_copy(out=spread[:], in_=bias_cols[:].unsqueeze(2).to_broadcast([P, BLOCKS, P]))
+
+        def bias_along_rows():
+            for s in range(S):
+                rows = psum3.tile([P, DS], F32, tag="turn")
+                for q in range(DS // P):
+                    nc.tensor.transpose(rows[:, P * q : P * (q + 1)], spread[:, (DS // P) * s + q, :], ident[:])
+                nc.scalar.copy(out=bias_rows[:, DS * s : DS * (s + 1)], in_=rows[:])
 
         def transpose(t):
             c, j = divmod(t, J)
             if j == 0:
-                if c + 1 < CHUNKS:
-                    load_state(c + 1)
+                if 2 <= c and c + 1 < CHUNKS:
+                    state_tiles(c + 1)
+                    load_a(c + 1)
+                    nc.sync.dma_start(out=h_tiles[c + 1][:], in_=h_chunks[c + 1])
                 at = psum2.tile([P, J, P], F32, tag="gt")
                 for jj in range(J):
                     nc.tensor.transpose(at[:, jj, :], a_tiles[c][:, jj, :].bitcast(F32), ident[:])
@@ -119,6 +160,10 @@ def tile_tpru_pb_t_kernel(tc, a, vr, h, x2g, w_g_words, w_g_scales, b_g, bg, out
             for g in range(G):
                 for u in range(2):
                     nc.tensor.transpose(ht[:, g, u, :], h_words[:, 256 * g + u : 256 * (g + 1) : 2], ident[:])
+            if t < FIRST:
+                grouped_tiles[(0, t)] = work.tile([P, G, P, 2], F32, name="grouped_first", align_bytes=64)
+                nc.scalar.copy(out=grouped_tiles[(0, t)][:], in_=ht[:].rearrange("p g u b -> p g b u"))
+                return
             if j == 0:
                 grouped_tiles[c] = sb.tile([P, G, ROWS, 2], F32, name="grouped", align_bytes=64)
             nc.scalar.copy(
@@ -133,6 +178,34 @@ def tile_tpru_pb_t_kernel(tc, a, vr, h, x2g, w_g_words, w_g_scales, b_g, bg, out
                 scales=scale_tiles[c][:].rearrange("p g b -> p (g b)"),
                 in_=grouped_tiles.pop(c)[:].rearrange("p g b u -> p (g b u)").bitcast(BF16),
             )
+
+        def quantise_first(t):
+            code_tiles[(0, t)] = sb.tile([P, G, P], U32, name="codes_first", align_bytes=64)
+            scale_tiles[(0, t)] = sb.tile([P, G, P], U8, name="scales_first", align_bytes=64)
+            nc.vector.quantize_mx(
+                out=code_tiles[(0, t)][:].rearrange("p g b -> p (g b)").bitcast(FP8X4),
+                scales=scale_tiles[(0, t)][:].rearrange("p g b -> p (g b)"),
+                in_=grouped_tiles.pop((0, t))[:].rearrange("p g b u -> p (g b u)").bitcast(BF16),
+            )
+
+        def biased_input(t, engine):
+            xb_tiles[t] = sb.tile([P, D], F32, name="xb", bufs=FIRST)
+            engine.tensor_tensor(out=xb_tiles[t][:], in0=x_tiles[0][:, t, :], in1=bias_rows[:], op=ALU.add)
+
+        def rows_matmuls(t):
+            for s in range(S):
+                zb = psum3.tile([P, DS], F32, tag="turn")
+                for g in range(G):
+                    nc.tensor.matmul_mx(
+                        out=zb[:],
+                        lhsT=code_tiles[(0, t)][:, g, :].bitcast(FP8X4),
+                        lhsT_scale=scale_tiles[(0, t)][:, g, :],
+                        rhs=w_words[:, g, 2 * DS * s : 2 * DS * (s + 1)].bitcast(FP4X4),
+                        rhs_scale=w_planes[:, g, DS * s : DS * (s + 1)],
+                        start=(g == 0),
+                        stop=(g == G - 1),
+                    )
+                zb_tiles[(t, s)] = zb
 
         def gate_matmuls(m):
             c, quarter = divmod(m, J)
@@ -180,11 +253,12 @@ def tile_tpru_pb_t_kernel(tc, a, vr, h, x2g, w_g_words, w_g_scales, b_g, bg, out
 
         def gate_sums(r):
             c, j = divmod(r, J)
+            added = xb_tiles.pop(r)[:] if r < FIRST else x_tiles[c][:, j, :]
             z = work.tile([P, D], F32, name="z")
             g_sb = work.tile([P, D], F32, name="g_sb")
-            nc.vector.tensor_tensor(out=z[:, first], in0=zb_tiles.pop((r, 0))[:], in1=x_tiles[c][:, j, first], op=ALU.add)
+            nc.vector.tensor_tensor(out=z[:, first], in0=zb_tiles.pop((r, 0))[:], in1=added[:, first], op=ALU.add)
             nc.scalar.activation(out=g_sb[:, first], in_=z[:, first], func=ACT.Sigmoid)
-            nc.vector.tensor_tensor(out=z[:, second], in0=zb_tiles.pop((r, 1))[:], in1=x_tiles[c][:, j, second], op=ALU.add)
+            nc.vector.tensor_tensor(out=z[:, second], in0=zb_tiles.pop((r, 1))[:], in1=added[:, second], op=ALU.add)
             nc.scalar.activation(out=g_sb[:, second], in_=z[:, second], func=ACT.Sigmoid, scale=-1.0)
             g_tiles[r] = g_sb
 
@@ -211,22 +285,34 @@ def tile_tpru_pb_t_kernel(tc, a, vr, h, x2g, w_g_words, w_g_scales, b_g, bg, out
                 nc.vector.tensor_tensor(out=o_sb[:, first], in0=move0[:], in1=h_tiles[c][:, j, first], op=ALU.add)
                 nc.sync.dma_start(out=out_chunks[c][j][:, first], in_=o_sb[:, first])
 
-        for r in range(-TRANSPOSE_AHEAD, ROW_TILES + 1):
+        for r in range(FIRST - TRANSPOSE_AHEAD, ROW_TILES + 1):
             if 0 <= r < ROW_TILES:
                 gate_sums(r)
-            if 0 <= r + QUANTISE_AHEAD < ROW_TILES and (r + QUANTISE_AHEAD) % J == J - 1:
+            if 0 <= r + QUANTISE_AHEAD_FIRST < FIRST:
+                quantise_first(r + QUANTISE_AHEAD_FIRST)
+                if r + QUANTISE_AHEAD_FIRST < 2:
+                    biased_input(r + QUANTISE_AHEAD_FIRST, nc.vector)
+            if FIRST <= r + QUANTISE_AHEAD < ROW_TILES and (r + QUANTISE_AHEAD) % J == J - 1:
                 quantise((r + QUANTISE_AHEAD) // J)
             if 0 <= r < ROW_TILES:
                 gate_rest(r)
             if 0 <= r - 1:
                 blend(r - 1)
-            if r + TRANSPOSE_AHEAD < ROW_TILES:
+            if 2 <= r + 3 < FIRST:
+                biased_input(r + 3, nc.gpsimd)
+            if FIRST <= r + TRANSPOSE_AHEAD < ROW_TILES:
                 transpose(r + TRANSPOSE_AHEAD)
-            if r + MATMUL_AHEAD == -1:
+            if 0 <= r + TRANSPOSE_AHEAD_FIRST < FIRST:
+                transpose(r + TRANSPOSE_AHEAD_FIRST)
+            if r == FIRST - TRANSPOSE_AHEAD + 1:
                 bias_columns()
-            if 0 <= r + 1 < ROW_TILES:
+            if r == FIRST - TRANSPOSE_AHEAD + 3:
+                bias_along_rows()
+            if 0 <= r + 1 < FIRST:
+                rows_matmuls(r + 1)
+            if FIRST <= r + 1 < ROW_TILES:
                 turn_back(r + 1)
-            if 0 <= r + MATMUL_AHEAD < ROW_TILES:
+            if FIRST <= r + MATMUL_AHEAD < ROW_TILES:
                 gate_matmuls(r + MATMUL_AHEAD)
             if 0 <= r + 1 < ROW_TILES:
                 roles_slice1(r + 1)

@@ -131,8 +131,13 @@ def tile_tpru_pb_t_kernel(tc, a, vr, h, x2g, w_g_words, w_g_scales, b_g, bg, out
         def bias_columns():
             b_cols = psum2.tile([P, P], F32, tag="gt")
             nc.tensor.transpose(b_cols[:], b_rows32[:], ident[:])
+            half = BLOCKS // S
             nc.vector.tensor_tensor(
-                out=bias_cols[:], in0=b_cols[:, 0:BLOCKS], in1=bg_rows[:].to_broadcast([P, BLOCKS]), op=ALU.add
+                out=bias_cols[:, 0:half], in0=b_cols[:, 0:half], in1=bg_rows[:].to_broadcast([P, half]), op=ALU.add
+            )
+            nc.vector.scalar_tensor_tensor(
+                out=bias_cols[:, half:BLOCKS], in0=b_cols[:, half:BLOCKS], scalar=-1.0,
+                in1=bg_rows[:].to_broadcast([P, half]), op0=ALU.mult, op1=ALU.subtract,
             )
             nc.vector.tensor_copy(out=spread[:], in_=bias_cols[:].unsqueeze(2).to_broadcast([P, BLOCKS, P]))
 
@@ -190,7 +195,10 @@ def tile_tpru_pb_t_kernel(tc, a, vr, h, x2g, w_g_words, w_g_scales, b_g, bg, out
 
         def biased_input(t, engine):
             xb_tiles[t] = sb.tile([P, D], F32, name="xb", bufs=FIRST)
-            engine.tensor_tensor(out=xb_tiles[t][:], in0=x_tiles[0][:, t, :], in1=bias_rows[:], op=ALU.add)
+            engine.tensor_tensor(out=xb_tiles[t][:, first], in0=x_tiles[0][:, t, first], in1=bias_rows[:, first], op=ALU.add)
+            engine.tensor_tensor(
+                out=xb_tiles[t][:, second], in0=bias_rows[:, second], in1=x_tiles[0][:, t, second], op=ALU.subtract
+            )
 
         def rows_matmuls(t):
             for s in range(S):
@@ -226,7 +234,8 @@ def tile_tpru_pb_t_kernel(tc, a, vr, h, x2g, w_g_words, w_g_scales, b_g, bg, out
                         stop=(g == G - 1),
                     )
                 nc.scalar.activation(
-                    out=zT_tiles[c][:, block, :], in_=gt[:], func=ACT.Identity, bias=bias_cols[:, block : block + 1]
+                    out=zT_tiles[c][:, block, :], in_=gt[:], func=ACT.Identity, bias=bias_cols[:, block : block + 1],
+                    scale=(1.0 if block < BLOCKS // S else -1.0),
                 )
 
         def turn_back(r):
@@ -257,9 +266,11 @@ def tile_tpru_pb_t_kernel(tc, a, vr, h, x2g, w_g_words, w_g_scales, b_g, bg, out
             z = work.tile([P, D], F32, name="z")
             g_sb = work.tile([P, D], F32, name="g_sb")
             nc.vector.tensor_tensor(out=z[:, first], in0=zb_tiles.pop((r, 0))[:], in1=added[:, first], op=ALU.add)
-            nc.scalar.activation(out=g_sb[:, first], in_=z[:, first], func=ACT.Sigmoid)
-            nc.vector.tensor_tensor(out=z[:, second], in0=zb_tiles.pop((r, 1))[:], in1=added[:, second], op=ALU.add)
-            nc.scalar.activation(out=g_sb[:, second], in_=z[:, second], func=ACT.Sigmoid, scale=-1.0)
+            if r < FIRST:
+                nc.vector.tensor_tensor(out=z[:, second], in0=added[:, second], in1=zb_tiles.pop((r, 1))[:], op=ALU.subtract)
+            else:
+                nc.vector.tensor_tensor(out=z[:, second], in0=zb_tiles.pop((r, 1))[:], in1=added[:, second], op=ALU.subtract)
+            nc.scalar.activation(out=g_sb[:], in_=z[:], func=ACT.Sigmoid)
             g_tiles[r] = g_sb
 
         def gate_rest(r):

@@ -29,6 +29,8 @@ MATMUL_AHEAD = 5
 FIRST = J
 TRANSPOSE_AHEAD_FIRST = 3
 QUANTISE_AHEAD_FIRST = 2
+LATE = ROW_TILES - 2 * J
+T4 = 4
 
 FLOPS = 2 * B * D * D + 2 * B * N * D
 
@@ -52,7 +54,7 @@ def tile_tpru_pb_t_kernel(tc, a, vr, h, x2g, w_g_words, w_g_scales, b_g, bg, out
 
         h_tiles, a_tiles, x_tiles, aT_tiles = {}, {}, {}, {}
         grouped_tiles, code_tiles, scale_tiles, zT_tiles = {}, {}, {}, {}
-        zb_tiles, diff0_tiles, hh1_tiles, g_tiles, back1_tiles, xb_tiles = {}, {}, {}, {}, {}, {}
+        zb_tiles, diff0_tiles, hh1_tiles, g_tiles, back1_tiles, xb_tiles, neg_tiles = {}, {}, {}, {}, {}, {}, {}
 
         def state_tiles(c):
             a_tiles[c] = sb.tile([P, J, N * S], BF16, name="a_sb", bufs=3)
@@ -122,6 +124,11 @@ def tile_tpru_pb_t_kernel(tc, a, vr, h, x2g, w_g_words, w_g_scales, b_g, bg, out
         load_h(2 * FIRST + 3)
         load_x_first(3)
 
+        vr1_by_t = const.tile([P, DS], BF16)
+        nc.gpsimd.tensor_copy(
+            out=vr1_by_t[:].rearrange("n (t p) -> n t p", t=T4), in_=vr_sb[:, 1, :].rearrange("n (p t) -> n t p", t=T4)
+        )
+
         b_rows32 = const.tile([P, P], F32)
         nc.vector.tensor_copy(out=b_rows32[:], in_=b_rows[:])
         bias_cols = const.tile([P, BLOCKS], F32)
@@ -181,7 +188,7 @@ def tile_tpru_pb_t_kernel(tc, a, vr, h, x2g, w_g_words, w_g_scales, b_g, bg, out
             nc.vector.quantize_mx(
                 out=code_tiles[c][:].rearrange("p g b -> p (g b)").bitcast(FP8X4),
                 scales=scale_tiles[c][:].rearrange("p g b -> p (g b)"),
-                in_=grouped_tiles.pop(c)[:].rearrange("p g b u -> p (g b u)").bitcast(BF16),
+                in_=grouped_tiles[c][:].rearrange("p g b u -> p (g b u)").bitcast(BF16),
             )
 
         def quantise_first(t):
@@ -248,10 +255,28 @@ def tile_tpru_pb_t_kernel(tc, a, vr, h, x2g, w_g_words, w_g_scales, b_g, bg, out
                     )
                 zb_tiles[(r, s)] = zb
 
+        def negate(r):
+            c, j = divmod(r, J)
+            neg_tiles[r] = work.tile([P, T4, P], F32, name="neg", bufs=2)
+            nc.scalar.activation(
+                out=neg_tiles[r][:],
+                in_=grouped_tiles[c][:, 1, P * j : P * (j + 1), :].bitcast(BF16).rearrange("p b t -> p t b"),
+                func=ACT.Copy, scale=-1.0,
+            )
+
         def roles_slice1(r):
             c, j = divmod(r, J)
             hh1_tiles[r] = psum2.tile([P, DS], F32, name="hh1")
-            nc.tensor.matmul(out=hh1_tiles[r][:], lhsT=aT_tiles[c][:, 1, j, :], rhs=vr_sb[:, 1, :], start=True, stop=True)
+            if r < LATE:
+                nc.tensor.matmul(out=hh1_tiles[r][:], lhsT=aT_tiles[c][:, 1, j, :], rhs=vr_sb[:, 1, :], start=True, stop=True)
+                return
+            nc.tensor.matmul(out=hh1_tiles[r][:], lhsT=aT_tiles[c][:, 1, j, :], rhs=vr1_by_t[:], start=True, stop=False)
+            neg = neg_tiles.pop(r)
+            for t in range(T4):
+                nc.tensor.matmul(
+                    out=hh1_tiles[r][:, P * t : P * (t + 1)], lhsT=neg[:, t, :], rhs=ident[:], is_transpose=True,
+                    start=False, stop=(t == T4 - 1),
+                )
 
         def roles_slice0(r):
             c, j = divmod(r, J)
@@ -266,7 +291,7 @@ def tile_tpru_pb_t_kernel(tc, a, vr, h, x2g, w_g_words, w_g_scales, b_g, bg, out
             z = work.tile([P, D], F32, name="z")
             g_sb = work.tile([P, D], F32, name="g_sb")
             nc.vector.tensor_tensor(out=z[:, first], in0=zb_tiles.pop((r, 0))[:], in1=added[:, first], op=ALU.add)
-            if r < FIRST:
+            if r < FIRST or r >= LATE:
                 nc.vector.tensor_tensor(out=z[:, second], in0=added[:, second], in1=zb_tiles.pop((r, 1))[:], op=ALU.subtract)
             else:
                 nc.vector.tensor_tensor(out=z[:, second], in0=zb_tiles.pop((r, 1))[:], in1=added[:, second], op=ALU.subtract)
@@ -274,6 +299,8 @@ def tile_tpru_pb_t_kernel(tc, a, vr, h, x2g, w_g_words, w_g_scales, b_g, bg, out
             g_tiles[r] = g_sb
 
         def gate_rest(r):
+            if r >= LATE:
+                return
             c, j = divmod(r, J)
             g_sb = g_tiles[r]
             diff1 = work.tile([P, DS], F32, name="diff1")
@@ -281,7 +308,33 @@ def tile_tpru_pb_t_kernel(tc, a, vr, h, x2g, w_g_words, w_g_scales, b_g, bg, out
             back1_tiles[r] = work.tile([P, DS], F32, name="back1")
             nc.gpsimd.tensor_tensor(out=back1_tiles[r][:], in0=g_sb[:, second], in1=diff1[:], op=ALU.mult)
 
+        def blend_late(r):
+            c, j = divmod(r, J)
+            o_sb = work.tile([P, D], F32, name="o_sb")
+            move = g_tiles.pop(r)
+            g_sb = move
+            last = r == ROW_TILES - 1
+            nc.vector.tensor_tensor(out=move[:, first], in0=diff0_tiles.pop(r)[:], in1=g_sb[:, first], op=ALU.mult)
+            if last:
+                nc.vector.tensor_tensor(out=o_sb[:, first], in0=move[:, first], in1=h_tiles[c][:, j, first], op=ALU.add)
+                nc.sync.dma_start(out=out_chunks[c][j][:, first], in_=o_sb[:, first])
+            nc.vector.tensor_tensor(
+                out=move[:, second].rearrange("b (p t) -> b p t", t=T4),
+                in0=hh1_tiles.pop(r)[:].rearrange("b (t p) -> b p t", t=T4),
+                in1=g_sb[:, second].rearrange("b (p t) -> b p t", t=T4),
+                op=ALU.mult,
+            )
+            if last:
+                nc.vector.tensor_tensor(out=o_sb[:, second], in0=move[:, second], in1=h_tiles[c][:, j, second], op=ALU.add)
+                nc.sync.dma_start(out=out_chunks[c][j][:, second], in_=o_sb[:, second])
+            else:
+                nc.gpsimd.tensor_tensor(out=o_sb[:], in0=move[:], in1=h_tiles[c][:, j, :], op=ALU.add)
+                nc.sync.dma_start(out=out_chunks[c][j], in_=o_sb[:])
+
         def blend(r):
+            if r >= LATE:
+                blend_late(r)
+                return
             c, j = divmod(r, J)
             o_sb = work.tile([P, D], F32, name="o_sb")
             move0 = work.tile([P, DS], F32, name="move0")
@@ -325,7 +378,11 @@ def tile_tpru_pb_t_kernel(tc, a, vr, h, x2g, w_g_words, w_g_scales, b_g, bg, out
                 turn_back(r + 1)
             if FIRST <= r + MATMUL_AHEAD < ROW_TILES:
                 gate_matmuls(r + MATMUL_AHEAD)
-            if 0 <= r + 1 < ROW_TILES:
+            if 0 <= r + 1 < LATE:
                 roles_slice1(r + 1)
+            if LATE <= r < ROW_TILES:
+                roles_slice1(r)
             if 0 <= r < ROW_TILES:
                 roles_slice0(r)
+            if LATE <= r + 2 < ROW_TILES:
+                negate(r + 2)

@@ -26,6 +26,7 @@ BLOCKS_A_TURN = BLOCKS // J
 TRANSPOSE_AHEAD = 10
 QUANTISE_AHEAD = 9
 MATMUL_AHEAD = 5
+ROLES_AHEAD = 6
 FIRST = J
 TRANSPOSE_AHEAD_FIRST = 3
 QUANTISE_AHEAD_FIRST = 2
@@ -90,7 +91,6 @@ def tile_tpru_pb_t_kernel(tc, a, vr, h, x2g, w_g_words, w_g_scales, b_g, bg, out
 
         for c in range(3):
             state_tiles(c)
-        load_a(1)
         load_h(FIRST)
         load_h(FIRST + 1)
         nc.sync.dma_start(out=b_rows[0:BLOCKS, :], in_=b_g.rearrange("(r c) -> r c", c=P))
@@ -110,7 +110,7 @@ def tile_tpru_pb_t_kernel(tc, a, vr, h, x2g, w_g_words, w_g_scales, b_g, bg, out
                 in_=w_g_scales[:, 4 * quad : 4 * quad + 4, :].rearrange("g r n -> r g n").bitcast(I32),
             )
         load_x_first(0)
-        load_a(2)
+        load_a(1)
         load_h(2 * FIRST)
         load_h(1)
         vr_sb = const.tile([P, S, DS], BF16)
@@ -120,6 +120,7 @@ def tile_tpru_pb_t_kernel(tc, a, vr, h, x2g, w_g_words, w_g_scales, b_g, bg, out
         load_x_first(1)
         load_h(2 * FIRST + 2)
         load_h(3)
+        load_a(2)
         load_x_first(2)
         load_h(2 * FIRST + 3)
         load_x_first(3)
@@ -155,6 +156,13 @@ def tile_tpru_pb_t_kernel(tc, a, vr, h, x2g, w_g_words, w_g_scales, b_g, bg, out
                     nc.tensor.transpose(rows[:, P * q : P * (q + 1)], spread[:, (DS // P) * s + q, :], ident[:])
                 nc.scalar.copy(out=bias_rows[:, DS * s : DS * (s + 1)], in_=rows[:])
 
+        def transpose_a(c):
+            at = psum2.tile([P, J, P], F32, tag="gt")
+            for jj in range(J):
+                nc.tensor.transpose(at[:, jj, :], a_tiles[c][:, jj, :].bitcast(F32), ident[:])
+            aT_tiles[c] = sb.tile([P, S, J, P], BF16, name="aT", bufs=4)
+            nc.scalar.copy(out=aT_tiles[c][:], in_=at[:].bitcast(BF16).rearrange("n j (b s) -> n s j b", s=S))
+
         def transpose(t):
             c, j = divmod(t, J)
             if j == 0:
@@ -162,11 +170,8 @@ def tile_tpru_pb_t_kernel(tc, a, vr, h, x2g, w_g_words, w_g_scales, b_g, bg, out
                     state_tiles(c + 1)
                     load_a(c + 1)
                     nc.sync.dma_start(out=h_tiles[c + 1][:], in_=h_chunks[c + 1])
-                at = psum2.tile([P, J, P], F32, tag="gt")
-                for jj in range(J):
-                    nc.tensor.transpose(at[:, jj, :], a_tiles[c][:, jj, :].bitcast(F32), ident[:])
-                aT_tiles[c] = sb.tile([P, S, J, P], BF16, name="aT", bufs=4)
-                nc.scalar.copy(out=aT_tiles[c][:], in_=at[:].bitcast(BF16).rearrange("n j (b s) -> n s j b", s=S))
+                if c == 0:
+                    transpose_a(c)
             h_words = h_tiles[c][:, j, :].bitcast(F32)
             ht = psum3.tile([P, G, 2, P], F32, tag="turn")
             for g in range(G):
@@ -310,7 +315,7 @@ def tile_tpru_pb_t_kernel(tc, a, vr, h, x2g, w_g_words, w_g_scales, b_g, bg, out
 
         def blend_late(r):
             c, j = divmod(r, J)
-            o_sb = work.tile([P, D], F32, name="o_sb")
+            o_sb = sb.tile([P, D], F32, name="xb", bufs=FIRST)
             move = g_tiles.pop(r)
             g_sb = move
             last = r == ROW_TILES - 1
@@ -364,6 +369,8 @@ def tile_tpru_pb_t_kernel(tc, a, vr, h, x2g, w_g_words, w_g_scales, b_g, bg, out
                 blend(r - 1)
             if 2 <= r + 3 < FIRST:
                 biased_input(r + 3, nc.gpsimd)
+            if FIRST <= r + ROLES_AHEAD < ROW_TILES and (r + ROLES_AHEAD) % J == 0:
+                transpose_a((r + ROLES_AHEAD) // J)
             if FIRST <= r + TRANSPOSE_AHEAD < ROW_TILES:
                 transpose(r + TRANSPOSE_AHEAD)
             if 0 <= r + TRANSPOSE_AHEAD_FIRST < FIRST:

from contextlib import ExitStack

import concourse.mybir as mybir
from concourse.masks import make_identity

F32 = mybir.dt.float32
BF16 = mybir.dt.bfloat16
I32 = mybir.dt.int32
U32 = mybir.dt.uint32
U8 = mybir.dt.uint8
FP8X4 = mybir.dt.float8_e4m3fn_x4
FP4X4 = mybir.dt.float4_e2m1fn_x4
ALU = mybir.AluOpType
ACT = mybir.ActivationFunctionType

B, D, S, N = 4096, 1024, 2, 128
DS = D // S
P = 128
G = D // 512
J = 4
ROWS = P * J
CHUNKS = B // ROWS
ROW_TILES = B // P
BLOCKS = D // P
BLOCKS_A_TURN = BLOCKS // J
TRANSPOSE_AHEAD = 10
QUANTISE_AHEAD = 9
MATMUL_AHEAD = 5
ROLES_AHEAD = 6
FIRST = J
TRANSPOSE_AHEAD_FIRST = 3
QUANTISE_AHEAD_FIRST = 2
LATE = ROW_TILES - 2 * J
T4 = 4

FLOPS = 2 * B * D * D + 2 * B * N * D


def tile_tpru_pb_t_kernel(tc, a, vr, h, x2g, w_g_words, w_g_scales, b_g, bg, out):
    nc = tc.nc
    h_chunks = h.rearrange("(c p j) k -> c p j k", p=P, j=J)
    x_chunks = x2g.rearrange("(c p j) k -> c p j k", p=P, j=J)
    a_chunks = a.rearrange("(c p j) n s -> c p j (n s)", p=P, j=J)
    out_chunks = out.rearrange("(c p j) k -> c j p k", p=P, j=J)
    first, second = slice(0, DS), slice(DS, D)

    with ExitStack() as ctx:
        const = ctx.enter_context(tc.tile_pool(name="const", bufs=1))
        sb = ctx.enter_context(tc.tile_pool(name="sb", bufs=2))
        work = ctx.enter_context(tc.tile_pool(name="work", bufs=3))
        psum2 = ctx.enter_context(tc.psum_pool(name="psum2", bufs=2))
        psum1 = ctx.enter_context(tc.psum_pool(name="psum1", bufs=1))
        psum3 = ctx.enter_context(tc.psum_pool(name="psum3", bufs=3))
        ctx.enter_context(tc.manual_schedule())

        h_tiles, a_tiles, x_tiles, aT_tiles = {}, {}, {}, {}
        grouped_tiles, code_tiles, scale_tiles, zT_tiles = {}, {}, {}, {}
        zb_tiles, diff0_tiles, hh1_tiles, g_tiles, back1_tiles, xb_tiles, neg_tiles = {}, {}, {}, {}, {}, {}, {}

        def state_tiles(c):
            a_tiles[c] = sb.tile([P, J, N * S], BF16, name="a_sb", bufs=3)
            h_tiles[c] = sb.tile([P, J, D], BF16, name="h_sb", bufs=5)

        def load_a(c):
            nc.sync.dma_start(out=a_tiles[c][:], in_=a_chunks[c])

        def load_h(t):
            c, j = divmod(t, J)
            nc.sync.dma_start(out=h_tiles[c][:, j, :], in_=h_chunks[c][:, j, :])

        def load_x_first(j):
            if j == 0:
                x_tiles[0] = sb.tile([P, J, D], BF16, name="x_sb", bufs=3)
            nc.sync.dma_start(out=x_tiles[0][:, j, :], in_=x_chunks[0][:, j, :])

        b_rows = const.tile([P, P], BF16)
        nc.vector.memset(b_rows[:], 0.0)
        w_planes = const.tile([P, G, D], U8, align_bytes=64)
        nc.vector.memset(w_planes[:].bitcast(I32), 0)
        ident = const.tile([P, P], F32)
        make_identity(nc, ident[:])
        ident_bf = const.tile([P, P], BF16)
        make_identity(nc, ident_bf[:])
        minus_ident = const.tile([P, P], BF16)
        nc.vector.tensor_scalar_mul(out=minus_ident[:], in0=ident_bf[:], scalar1=-1.0)

        zero_col = const.tile([P, 1], F32)
        nc.vector.memset(zero_col[:], 0.0)
        half_col = const.tile([P, 1], F32)
        nc.scalar.activation(out=half_col[:], in_=zero_col[:], func=ACT.Sigmoid)

        for c in range(3):
            state_tiles(c)
        load_h(FIRST)
        load_h(FIRST + 1)
        nc.sync.dma_start(out=b_rows[0:BLOCKS, :], in_=b_g.rearrange("(r c) -> r c", c=P))
        bg_rows = const.tile([P, 1], BF16)
        nc.sync.dma_start(out=bg_rows[:], in_=bg.partition_broadcast(P))
        load_h(FIRST + 2)
        load_h(FIRST + 3)
        load_a(0)
        load_h(0)
        w_words = const.tile([P, G, 2 * D], U8, align_bytes=64)
        nc.sync.dma_start(
            out=w_words[:].bitcast(I32), in_=w_g_words.rearrange("g p c -> p g c").bitcast(I32)
        )
        for quad in range(4):
            nc.sync.dma_start(
                out=w_planes[32 * quad : 32 * quad + 4].bitcast(I32),
                in_=w_g_scales[:, 4 * quad : 4 * quad + 4, :].rearrange("g r n -> r g n").bitcast(I32),
            )
        load_x_first(0)
        load_a(1)
        load_h(2 * FIRST)
        load_h(1)
        vr_sb = const.tile([P, S, DS], BF16)
        nc.sync.dma_start(out=vr_sb[:], in_=vr)
        load_h(2 * FIRST + 1)
        load_h(2)
        load_x_first(1)
        load_h(2 * FIRST + 2)
        load_h(3)
        load_a(2)
        load_x_first(2)
        load_h(2 * FIRST + 3)
        load_x_first(3)

        vr1_by_t = const.tile([P, DS], BF16)
        nc.gpsimd.tensor_copy(
            out=vr1_by_t[:].rearrange("n (t p) -> n t p", t=T4), in_=vr_sb[:, 1, :].rearrange("n (p t) -> n t p", t=T4)
        )

        b_rows32 = const.tile([P, P], F32)
        nc.vector.tensor_copy(out=b_rows32[:], in_=b_rows[:])
        bias_cols = const.tile([P, BLOCKS], F32)
        bias_rows = const.tile([P, D], F32)
        spread = const.tile([P, BLOCKS, P], F32)

        def bias_columns():
            b_cols = psum2.tile([P, P], F32, tag="gt")
            nc.tensor.transpose(b_cols[:], b_rows32[:], ident[:])
            half = BLOCKS // S
            nc.vector.tensor_tensor(
                out=bias_cols[:, 0:half], in0=b_cols[:, 0:half], in1=bg_rows[:].to_broadcast([P, half]), op=ALU.add
            )
            nc.vector.scalar_tensor_tensor(
                out=bias_cols[:, half:BLOCKS], in0=b_cols[:, half:BLOCKS], scalar=-1.0,
                in1=bg_rows[:].to_broadcast([P, half]), op0=ALU.mult, op1=ALU.subtract,
            )
            nc.vector.tensor_copy(out=spread[:], in_=bias_cols[:].unsqueeze(2).to_broadcast([P, BLOCKS, P]))

        def bias_along_rows():
            for s in range(S):
                rows = psum3.tile([P, DS], F32, tag="turn")
                for q in range(DS // P):
                    nc.tensor.transpose(rows[:, P * q : P * (q + 1)], spread[:, (DS // P) * s + q, :], ident[:])
                nc.scalar.copy(out=bias_rows[:, DS * s : DS * (s + 1)], in_=rows[:])

        def transpose_a(c):
            at = psum2.tile([P, J, P], F32, tag="gt")
            for jj in range(J):
                nc.tensor.transpose(at[:, jj, :], a_tiles[c][:, jj, :].bitcast(F32), ident[:])
            aT_tiles[c] = sb.tile([P, S, J, P], BF16, name="aT", bufs=4)
            nc.scalar.copy(out=aT_tiles[c][:], in_=at[:].bitcast(BF16).rearrange("n j (b s) -> n s j b", s=S))

        def transpose(t):
            c, j = divmod(t, J)
            if j == 0:
                if 2 <= c and c + 1 < CHUNKS:
                    state_tiles(c + 1)
                    load_a(c + 1)
                    nc.sync.dma_start(out=h_tiles[c + 1][:], in_=h_chunks[c + 1])
                if c == 0:
                    transpose_a(c)
            h_words = h_tiles[c][:, j, :].bitcast(F32)
            ht = psum3.tile([P, G, 2, P], F32, tag="turn")
            for g in range(G):
                for u in range(2):
                    nc.tensor.transpose(ht[:, g, u, :], h_words[:, 256 * g + u : 256 * (g + 1) : 2], ident[:])
            if t < FIRST:
                grouped_tiles[(0, t)] = work.tile([P, G, P, 2], F32, name="grouped_first", align_bytes=64)
                nc.scalar.copy(out=grouped_tiles[(0, t)][:], in_=ht[:].rearrange("p g u b -> p g b u"))
                return
            if j == 0:
                grouped_tiles[c] = sb.tile([P, G, ROWS, 2], F32, name="grouped", align_bytes=64)
            nc.scalar.copy(
                out=grouped_tiles[c][:, :, P * j : P * (j + 1), :], in_=ht[:].rearrange("p g u b -> p g b u")
            )

        def quantise(c):
            code_tiles[c] = sb.tile([P, G, ROWS], U32, name="codes", align_bytes=64)
            scale_tiles[c] = sb.tile([P, G, ROWS], U8, name="scales", align_bytes=64)
            nc.vector.quantize_mx(
                out=code_tiles[c][:].rearrange("p g b -> p (g b)").bitcast(FP8X4),
                scales=scale_tiles[c][:].rearrange("p g b -> p (g b)"),
                in_=grouped_tiles[c][:].rearrange("p g b u -> p (g b u)").bitcast(BF16),
            )

        def quantise_first(t):
            code_tiles[(0, t)] = sb.tile([P, G, P], U32, name="codes_first", align_bytes=64)
            scale_tiles[(0, t)] = sb.tile([P, G, P], U8, name="scales_first", align_bytes=64)
            nc.vector.quantize_mx(
                out=code_tiles[(0, t)][:].rearrange("p g b -> p (g b)").bitcast(FP8X4),
                scales=scale_tiles[(0, t)][:].rearrange("p g b -> p (g b)"),
                in_=grouped_tiles.pop((0, t))[:].rearrange("p g b u -> p (g b u)").bitcast(BF16),
            )

        def biased_input(t, engine):
            xb_tiles[t] = sb.tile([P, D], F32, name="xb", bufs=FIRST)
            engine.tensor_tensor(out=xb_tiles[t][:, first], in0=x_tiles[0][:, t, first], in1=bias_rows[:, first], op=ALU.add)
            engine.tensor_tensor(
                out=xb_tiles[t][:, second], in0=bias_rows[:, second], in1=x_tiles[0][:, t, second], op=ALU.subtract
            )

        def rows_matmuls(t):
            for s in range(S):
                zb = psum3.tile([P, DS], F32, tag="turn")
                for g in range(G):
                    nc.tensor.matmul_mx(
                        out=zb[:],
                        lhsT=code_tiles[(0, t)][:, g, :].bitcast(FP8X4),
                        lhsT_scale=scale_tiles[(0, t)][:, g, :],
                        rhs=w_words[:, g, 2 * DS * s : 2 * DS * (s + 1)].bitcast(FP4X4),
                        rhs_scale=w_planes[:, g, DS * s : DS * (s + 1)],
                        start=(g == 0),
                        stop=(g == G - 1),
                    )
                zb_tiles[(t, s)] = zb

        def gate_matmuls(m):
            c, quarter = divmod(m, J)
            if quarter == 0:
                x_tiles[c] = sb.tile([P, J, D], BF16, name="x_sb", bufs=3)
                nc.sync.dma_start(out=x_tiles[c][:], in_=x_chunks[c])
                zT_tiles[c] = sb.tile([P, BLOCKS, ROWS], F32, name="zT")
            for block in range(BLOCKS_A_TURN * quarter, BLOCKS_A_TURN * (quarter + 1)):
                gt = psum2.tile([P, ROWS], F32, tag="gt")
                for g in range(G):
                    nc.tensor.matmul_mx(
                        out=gt[:],
                        lhsT=w_words[:, g, 2 * P * block : 2 * P * (block + 1)].bitcast(FP4X4),
                        lhsT_scale=w_planes[:, g, P * block : P * (block + 1)],
                        rhs=code_tiles[c][:, g, :].bitcast(FP8X4),
                        rhs_scale=scale_tiles[c][:, g, :],
                        start=(g == 0),
                        stop=(g == G - 1),
                    )
                nc.scalar.activation(
                    out=zT_tiles[c][:, block, :], in_=gt[:], func=ACT.Identity, bias=bias_cols[:, block : block + 1],
                    scale=(1.0 if block < BLOCKS // S else -1.0),
                )

        def turn_back(r):
            c, j = divmod(r, J)
            for s in range(S):
                zb = psum3.tile([P, DS], F32, tag="turn")
                for q in range(DS // P):
                    nc.tensor.transpose(
                        zb[:, P * q : P * (q + 1)], zT_tiles[c][:, (DS // P) * s + q, P * j : P * (j + 1)], ident[:]
                    )
                zb_tiles[(r, s)] = zb

        def negate(r):
            c, j = divmod(r, J)
            neg_tiles[r] = work.tile([P, T4, P], F32, name="neg", bufs=2)
            nc.scalar.activation(
                out=neg_tiles[r][:],
                in_=grouped_tiles[c][:, 1, P * j : P * (j + 1), :].bitcast(BF16).rearrange("p b t -> p t b"),
                func=ACT.Copy, scale=-1.0,
            )

        def roles_slice1(r):
            c, j = divmod(r, J)
            hh1_tiles[r] = psum2.tile([P, DS], F32, name="hh1")
            if r < LATE:
                nc.tensor.matmul(out=hh1_tiles[r][:], lhsT=aT_tiles[c][:, 1, j, :], rhs=vr_sb[:, 1, :], start=True, stop=True)
                return
            nc.tensor.matmul(out=hh1_tiles[r][:], lhsT=aT_tiles[c][:, 1, j, :], rhs=vr1_by_t[:], start=True, stop=False)
            neg = neg_tiles.pop(r)
            for t in range(T4):
                nc.tensor.matmul(
                    out=hh1_tiles[r][:, P * t : P * (t + 1)], lhsT=neg[:, t, :], rhs=ident[:], is_transpose=True,
                    start=False, stop=(t == T4 - 1),
                )

        def roles_slice0(r):
            c, j = divmod(r, J)
            diff0 = psum1.tile([P, DS], F32, name="diff0")
            nc.tensor.matmul(out=diff0[:], lhsT=aT_tiles[c][:, 0, j, :], rhs=vr_sb[:, 0, :], start=True, stop=False)
            nc.tensor.matmul(out=diff0[:], lhsT=minus_ident[:], rhs=h_tiles[c][:, j, first], start=False, stop=True)
            diff0_tiles[r] = diff0

        def gate_sums(r):
            c, j = divmod(r, J)
            added = xb_tiles.pop(r)[:] if r < FIRST else x_tiles[c][:, j, :]
            z = work.tile([P, D], F32, name="z")
            g_sb = work.tile([P, D], F32, name="g_sb")
            nc.vector.tensor_tensor(out=z[:, first], in0=zb_tiles.pop((r, 0))[:], in1=added[:, first], op=ALU.add)
            if r < FIRST or r >= LATE:
                nc.vector.tensor_tensor(out=z[:, second], in0=added[:, second], in1=zb_tiles.pop((r, 1))[:], op=ALU.subtract)
            else:
                nc.vector.tensor_tensor(out=z[:, second], in0=zb_tiles.pop((r, 1))[:], in1=added[:, second], op=ALU.subtract)
            nc.scalar.activation(out=g_sb[:], in_=z[:], func=ACT.Sigmoid)
            g_tiles[r] = g_sb

        def gate_rest(r):
            if r >= LATE:
                return
            c, j = divmod(r, J)
            g_sb = g_tiles[r]
            diff1 = work.tile([P, DS], F32, name="diff1")
            nc.vector.tensor_tensor(out=diff1[:], in0=hh1_tiles[r][:], in1=h_tiles[c][:, j, second], op=ALU.subtract)
            back1_tiles[r] = work.tile([P, DS], F32, name="back1")
            nc.gpsimd.tensor_tensor(out=back1_tiles[r][:], in0=g_sb[:, second], in1=diff1[:], op=ALU.mult)

        def blend_late(r):
            c, j = divmod(r, J)
            o_sb = sb.tile([P, D], F32, name="xb", bufs=FIRST)
            move = g_tiles.pop(r)
            g_sb = move
            last = r == ROW_TILES - 1
            nc.vector.tensor_tensor(out=move[:, first], in0=diff0_tiles.pop(r)[:], in1=g_sb[:, first], op=ALU.mult)
            if last:
                nc.vector.tensor_tensor(out=o_sb[:, first], in0=move[:, first], in1=h_tiles[c][:, j, first], op=ALU.add)
                nc.sync.dma_start(out=out_chunks[c][j][:, first], in_=o_sb[:, first])
            nc.vector.tensor_tensor(
                out=move[:, second].rearrange("b (p t) -> b p t", t=T4),
                in0=hh1_tiles.pop(r)[:].rearrange("b (t p) -> b p t", t=T4),
                in1=g_sb[:, second].rearrange("b (p t) -> b p t", t=T4),
                op=ALU.mult,
            )
            if last:
                nc.vector.tensor_tensor(out=o_sb[:, second], in0=move[:, second], in1=h_tiles[c][:, j, second], op=ALU.add)
                nc.sync.dma_start(out=out_chunks[c][j][:, second], in_=o_sb[:, second])
            else:
                nc.gpsimd.tensor_tensor(out=o_sb[:], in0=move[:], in1=h_tiles[c][:, j, :], op=ALU.add)
                nc.sync.dma_start(out=out_chunks[c][j], in_=o_sb[:])

        def blend(r):
            if r >= LATE:
                blend_late(r)
                return
            c, j = divmod(r, J)
            o_sb = work.tile([P, D], F32, name="o_sb")
            move0 = work.tile([P, DS], F32, name="move0")
            nc.vector.tensor_tensor(out=move0[:], in0=diff0_tiles.pop(r)[:], in1=g_tiles.pop(r)[:, first], op=ALU.mult)
            if r < ROW_TILES - 1:
                nc.gpsimd.tensor_tensor(out=o_sb[:, first], in0=move0[:], in1=h_tiles[c][:, j, first], op=ALU.add)
            nc.vector.tensor_tensor(out=o_sb[:, second], in0=hh1_tiles.pop(r)[:], in1=back1_tiles.pop(r)[:], op=ALU.subtract)
            if r < ROW_TILES - 1:
                nc.sync.dma_start(out=out_chunks[c][j], in_=o_sb[:])
            else:
                nc.sync.dma_start(out=out_chunks[c][j][:, second], in_=o_sb[:, second])
                nc.vector.tensor_tensor(out=o_sb[:, first], in0=move0[:], in1=h_tiles[c][:, j, first], op=ALU.add)
                nc.sync.dma_start(out=out_chunks[c][j][:, first], in_=o_sb[:, first])

        for r in range(FIRST - TRANSPOSE_AHEAD, ROW_TILES + 1):
            if 0 <= r < ROW_TILES:
                gate_sums(r)
            if 0 <= r + QUANTISE_AHEAD_FIRST < FIRST:
                quantise_first(r + QUANTISE_AHEAD_FIRST)
                if r + QUANTISE_AHEAD_FIRST < 2:
                    biased_input(r + QUANTISE_AHEAD_FIRST, nc.vector)
            if FIRST <= r + QUANTISE_AHEAD < ROW_TILES and (r + QUANTISE_AHEAD) % J == J - 1:
                quantise((r + QUANTISE_AHEAD) // J)
            if 0 <= r < ROW_TILES:
                gate_rest(r)
            if 0 <= r - 1:
                blend(r - 1)
            if 2 <= r + 3 < FIRST:
                biased_input(r + 3, nc.gpsimd)
            if FIRST <= r + ROLES_AHEAD < ROW_TILES and (r + ROLES_AHEAD) % J == 0:
                transpose_a((r + ROLES_AHEAD) // J)
            if FIRST <= r + TRANSPOSE_AHEAD < ROW_TILES:
                transpose(r + TRANSPOSE_AHEAD)
            if 0 <= r + TRANSPOSE_AHEAD_FIRST < FIRST:
                transpose(r + TRANSPOSE_AHEAD_FIRST)
            if r == FIRST - TRANSPOSE_AHEAD + 1:
                bias_columns()
            if r == FIRST - TRANSPOSE_AHEAD + 3:
                bias_along_rows()
            if 0 <= r + 1 < FIRST:
                rows_matmuls(r + 1)
            if FIRST <= r + 1 < ROW_TILES:
                turn_back(r + 1)
            if FIRST <= r + MATMUL_AHEAD < ROW_TILES:
                gate_matmuls(r + MATMUL_AHEAD)
            if 0 <= r + 1 < LATE:
                roles_slice1(r + 1)
            if LATE <= r < ROW_TILES:
                roles_slice1(r)
            if 0 <= r < ROW_TILES:
                roles_slice0(r)
            if LATE <= r + 2 < ROW_TILES:
                negate(r + 2)
